import numpy as np
import ml_dtypes


def mxq(x, axis, fmt="e4m3"):
    dtype, down = {"e4m3": (ml_dtypes.float8_e4m3fn, 7), "e5m2": (ml_dtypes.float8_e5m2, 14)}[fmt]
    v = np.moveaxis(np.asarray(x, np.float32).astype(ml_dtypes.bfloat16).astype(np.float64), axis, -1)
    blocks = v.reshape(v.shape[:-1] + (-1, 32))
    amax = np.abs(blocks).max(-1, keepdims=True)
    byte = np.maximum(np.where(amax > 0, np.frexp(amax)[1] - 1 + 127, 0) - down, 1)
    scale = np.exp2(byte - 127.0)
    codes = (blocks / scale).astype(np.float32).astype(dtype).astype(np.float64)
    return np.moveaxis((codes * scale).reshape(v.shape), -1, axis)


WIDE = False


def mx_kscale(k):
    if not WIDE:
        return np.ones(k)
    levels = np.array([10, -10, 5, -5, 0])
    a = np.random.permutation(np.resize(levels, k // 512 * 4)).reshape(k // 512, 4)
    idx = np.arange(k)
    return np.exp2(a[idx // 512, idx % 128 // 32])


BF16 = ml_dtypes.bfloat16


def bf(x):
    return np.asarray(x, np.float32).astype(BF16)


def f64(x):
    return np.asarray(x).astype(np.float64)


T, B, D, M = 128, 128, 512, 128
TEMP = 0.1
QS = 0.3
SC = 2.0
MS = SC * TEMP / (QS * np.sqrt(D))


def setup_inputs():
    s = mx_kscale(D)
    return {"queries": bf(np.random.standard_normal((T, B, D)) * QS / s),
            "memory_items": bf(np.random.standard_normal((M, D)) * MS * s)}


def reference(queries, memory_items):
    q = f64(queries).reshape(T * B, D)
    mem = f64(memory_items)
    scores = ((mxq(q, 1, "e4m3") @ mxq(mem, 1, "e4m3").T) / TEMP).reshape(T, B, M)
    e = np.exp(scores - scores.max(0, keepdims=True))
    v_att = e / e.sum(0, keepdims=True)
    v = v_att.reshape(T * B, M)
    return (mxq(v, 0, "e4m3").T @ mxq(q, 0, "e4m3")) / B

@@ -1,0 +1,165 @@
+import concourse.mybir as mybir
+from concourse.masks import make_identity
+
+F32 = mybir.dt.float32
+BF16 = mybir.dt.bfloat16
+U32 = mybir.dt.uint32
+U8 = mybir.dt.uint8
+FP8X4 = mybir.dt.float8_e4m3fn_x4
+ALU = mybir.AluOpType
+ACT = mybir.ActivationFunctionType
+AXIS = mybir.AxisListType
+
+P = 128
+PACK = 4
+T, B, D, M = 128, 128, 512, 128
+TEMP = 0.1
+CHUNKS = T // PACK
+HALVES = 2
+SLOT_GROUP = 16
+SCALAR_REGROUP_EVERY = 3
+
+FLOPS = 2 * 2 * T * B * D * M
+
+
+def transpose_words(nc, bank, rows_bf16, ident):
+    words = rows_bf16.bitcast(F32)
+    for u in range(HALVES):
+        nc.tensor.transpose(bank[:, u, :], words[:, u * P : (u + 1) * P], ident[:])
+
+
+def tile_gatedmemorymodule_pa_kernel(tc, queries, memory_items, out):
+    nc = tc.nc
+    with tc.tile_pool(name="keep", bufs=1) as keep, tc.psum_pool(name="psum_t", bufs=4) as psum_t, tc.psum_pool(
+        name="psum_s", bufs=2
+    ) as psum_s, tc.psum_pool(name="psum_o", bufs=1) as psum_o:
+        ident = keep.tile([P, P], F32)
+        make_identity(nc, ident[:])
+
+        scores = keep.tile([P, CHUNKS, M, PACK], F32)
+        q2_codes = keep.tile([P, CHUNKS, D], U32, align_bytes=64)
+        q2_scales = keep.tile([P, CHUNKS, D], U8, align_bytes=64)
+        mem_codes = keep.tile([P, M], U32, align_bytes=64)
+        mem_scales = keep.tile([P, M], U8, align_bytes=64)
+        running_max = keep.tile([P, M, PACK], F32)
+
+        with tc.tile_pool(name="stage", bufs=3) as stage, tc.tile_pool(name="loads", bufs=6) as loads:
+            mem_raw = stage.tile([P, D], BF16)
+            nc.sync.dma_start(out=mem_raw[:], in_=memory_items)
+            mem_bank = psum_t.tile([P, HALVES, M], F32, tag="bank")
+            transpose_words(nc, mem_bank, mem_raw[:], ident)
+            mem_grouped = stage.tile([P, M, PACK], BF16, align_bytes=64)
+            nc.vector.tensor_copy(
+                out=mem_grouped[:].bitcast(F32), in_=mem_bank[:].rearrange("p u m -> p m u")
+            )
+            nc.vector.quantize_mx(
+                out=mem_codes[:].bitcast(FP8X4),
+                scales=mem_scales[:],
+                in_=mem_grouped[:].rearrange("p m k -> p (m k)"),
+            )
+
+            for c in range(CHUNKS):
+                raw = loads.tile([P, PACK, D], BF16)
+                nc.sync.dma_start(
+                    out=raw[:], in_=queries[c * PACK : (c + 1) * PACK].rearrange("t b d -> b t d")
+                )
+
+                q1_grouped = stage.tile([P, PACK, B, PACK], BF16, align_bytes=64)
+                q1_words = q1_grouped[:].bitcast(F32)
+                for pair in range(PACK // 2):
+                    bank = psum_t.tile([P, 2, HALVES, B], F32, tag="bank")
+                    for i in range(2):
+                        transpose_words(nc, bank[:, i], raw[:, 2 * pair + i, :], ident)
+                    nc.scalar.copy(
+                        out=q1_words[:, 2 * pair : 2 * pair + 2],
+                        in_=bank[:].rearrange("p i u b -> p i b u"),
+                    )
+                q1_codes = stage.tile([P, PACK * B], U32, align_bytes=64)
+                q1_scales = stage.tile([P, PACK * B], U8, align_bytes=64)
+                nc.vector.quantize_mx(
+                    out=q1_codes[:].bitcast(FP8X4),
+                    scales=q1_scales[:],
+                    in_=q1_grouped[:].rearrange("p t b k -> p (t b k)"),
+                )
+                score_bank = psum_s.tile([P, PACK, M], F32)
+                for j in range(PACK):
+                    nc.tensor.matmul_mx(
+                        out=score_bank[:, j, :],
+                        lhsT=q1_codes[:, j * B : (j + 1) * B].bitcast(FP8X4),
+                        lhsT_scale=q1_scales[:, j * B : (j + 1) * B],
+                        rhs=mem_codes[:].bitcast(FP8X4),
+                        rhs_scale=mem_scales[:],
+                        start=True,
+                        stop=True,
+                    )
+                nc.scalar.copy(out=scores[:, c], in_=score_bank[:].rearrange("p j m -> p m j"))
+                if c == 0:
+                    nc.vector.tensor_copy(out=running_max[:], in_=scores[:, c])
+                else:
+                    nc.vector.tensor_tensor(
+                        out=running_max[:], in0=running_max[:], in1=scores[:, c], op=ALU.max
+                    )
+
+                q2_grouped = stage.tile([P, D, PACK], BF16, align_bytes=64)
+                dst = q2_grouped[:].rearrange("p (c i) t -> p c t i", i=4)
+                src = raw[:].rearrange("p t (c i) -> p c t i", i=4)
+                if c % SCALAR_REGROUP_EVERY == SCALAR_REGROUP_EVERY - 1:
+                    nc.scalar.copy(out=dst, in_=src)
+                else:
+                    nc.vector.tensor_copy(out=dst, in_=src)
+                nc.vector.quantize_mx(
+                    out=q2_codes[:, c, :].bitcast(FP8X4),
+                    scales=q2_scales[:, c, :],
+                    in_=q2_grouped[:].rearrange("p d t -> p (d t)"),
+                )
+
+        with tc.tile_pool(name="soft", bufs=1) as soft:
+            neg_max = soft.tile([P, M], F32)
+            nc.vector.tensor_reduce(out=neg_max[:], in_=running_max[:], axis=AXIS.X, op=ALU.max)
+            nc.vector.tensor_scalar_mul(out=neg_max[:], in0=neg_max[:], scalar1=-1.0 / TEMP)
+            total = soft.tile([P, M], F32)
+            inverse = soft.tile([P, M], F32)
+            v_att = soft.tile([P, CHUNKS, M, PACK], BF16, align_bytes=64)
+            v_codes = soft.tile([P, CHUNKS, M], U32, align_bytes=64)
+            v_scales = soft.tile([P, CHUNKS, M], U8, align_bytes=64)
+            for g in range(M // SLOT_GROUP):
+                slots = slice(g * SLOT_GROUP, (g + 1) * SLOT_GROUP)
+                for m in range(g * SLOT_GROUP, (g + 1) * SLOT_GROUP):
+                    nc.scalar.activation(
+                        out=scores[:, :, m, :],
+                        in_=scores[:, :, m, :],
+                        func=ACT.Exp,
+                        bias=neg_max[:, m : m + 1],
+                        scale=1.0 / TEMP,
+                        accum_out=total[:, m : m + 1],
+                    )
+                nc.vector.reciprocal(out=inverse[:, slots], in_=total[:, slots])
+                nc.vector.tensor_tensor(
+                    out=v_att[:, :, slots, :],
+                    in0=scores[:, :, slots, :],
+                    in1=inverse[:, slots].unsqueeze(1).unsqueeze(3).to_broadcast([P, CHUNKS, SLOT_GROUP, PACK]),
+                    op=ALU.mult,
+                )
+
+            acc = psum_o.tile([P, D], F32)
+            wide = 8
+            for q in range(CHUNKS // wide):
+                part = slice(q * wide, (q + 1) * wide)
+                nc.vector.quantize_mx(
+                    out=v_codes[:, part, :].rearrange("p c m -> p (c m)").bitcast(FP8X4),
+                    scales=v_scales[:, part, :].rearrange("p c m -> p (c m)"),
+                    in_=v_att[:, part].rearrange("p c m t -> p (c m t)"),
+                )
+            for c in range(CHUNKS):
+                nc.tensor.matmul_mx(
+                    out=acc[:],
+                    lhsT=v_codes[:, c, :].bitcast(FP8X4),
+                    lhsT_scale=v_scales[:, c, :],
+                    rhs=q2_codes[:, c, :].bitcast(FP8X4),
+                    rhs_scale=q2_scales[:, c, :],
+                    start=(c == 0),
+                    stop=(c == CHUNKS - 1),
+                )
+            result = soft.tile([P, D], F32)
+            nc.scalar.mul(out=result[:], in_=acc[:], mul=1.0 / B)
+            nc.sync.dma_start(out=out, in_=result[:])

@@ -17,6 +17,13 @@ TEMP = 0.1
 CHUNKS = T // PACK
 HALVES = 2
 SLOT_GROUP = 16
+GROUPS = M // SLOT_GROUP
+WIDE = 8
+
+AT_THE_BARRIER = 1
+BESIDE_EXP = 3
+AT_THE_END = 6
+SHARED = CHUNKS - AT_THE_BARRIER - BESIDE_EXP - AT_THE_END
 SCALAR_REGROUP_EVERY = 3
 
 FLOPS = 2 * 2 * T * B * D * M
@@ -30,9 +37,15 @@ def transpose_words(nc, bank, rows_bf16, ident):
 
 def tile_gatedmemorymodule_pa_kernel(tc, queries, memory_items, out):
     nc = tc.nc
-    with tc.tile_pool(name="keep", bufs=1) as keep, tc.psum_pool(name="psum_t", bufs=4) as psum_t, tc.psum_pool(
-        name="psum_s", bufs=2
-    ) as psum_s, tc.psum_pool(name="psum_o", bufs=1) as psum_o:
+    with tc.tile_pool(name="keep", bufs=1) as keep, tc.tile_pool(name="loads", bufs=4) as loads, tc.tile_pool(
+        name="stage2", bufs=3
+    ) as stage2, tc.psum_pool(name="psum_t", bufs=4) as psum_t, tc.psum_pool(name="psum_s", bufs=2) as psum_s, tc.psum_pool(
+        name="psum_o", bufs=1
+    ) as psum_o:
+        warm = keep.tile([P, 1], F32)
+        nc.vector.memset(warm[:], 0.0)
+        nc.scalar.activation(out=warm[:], in_=warm[:], func=ACT.Exp)
+
         ident = keep.tile([P, P], F32)
         make_identity(nc, ident[:])
 
@@ -41,17 +54,35 @@ def tile_gatedmemorymodule_pa_kernel(tc, queries, memory_items, out):
         q2_scales = keep.tile([P, CHUNKS, D], U8, align_bytes=64)
         mem_codes = keep.tile([P, M], U32, align_bytes=64)
         mem_scales = keep.tile([P, M], U8, align_bytes=64)
-        running_max = keep.tile([P, M, PACK], F32)
+        running_max = keep.tile([P, 2, M, PACK], F32)
 
-        with tc.tile_pool(name="stage", bufs=3) as stage, tc.tile_pool(name="loads", bufs=6) as loads:
-            mem_raw = stage.tile([P, D], BF16)
+        def load_chunk(c):
+            raw = loads.tile([P, PACK, D], BF16, name="raw")
+            nc.sync.dma_start(out=raw[:], in_=queries[c * PACK : (c + 1) * PACK].rearrange("t b d -> b t d"))
+            return raw
+
+        def regroup(raw, copy):
+            q2_grouped = stage2.tile([P, D, PACK], BF16, align_bytes=64, name="q2_grouped")
+            copy(
+                out=q2_grouped[:].rearrange("p (c i) t -> p c t i", i=4),
+                in_=raw[:].rearrange("p t (c i) -> p c t i", i=4),
+            )
+            return q2_grouped
+
+        def quantise_q2(c, q2_grouped):
+            nc.vector.quantize_mx(
+                out=q2_codes[:, c, :].bitcast(FP8X4),
+                scales=q2_scales[:, c, :],
+                in_=q2_grouped[:].rearrange("p d t -> p (d t)"),
+            )
+
+        with tc.tile_pool(name="stage1", bufs=3) as stage1:
+            mem_raw = stage1.tile([P, D], BF16, bufs=1)
             nc.sync.dma_start(out=mem_raw[:], in_=memory_items)
             mem_bank = psum_t.tile([P, HALVES, M], F32, tag="bank")
             transpose_words(nc, mem_bank, mem_raw[:], ident)
-            mem_grouped = stage.tile([P, M, PACK], BF16, align_bytes=64)
-            nc.vector.tensor_copy(
-                out=mem_grouped[:].bitcast(F32), in_=mem_bank[:].rearrange("p u m -> p m u")
-            )
+            mem_grouped = stage1.tile([P, M, PACK], BF16, align_bytes=64, bufs=1)
+            nc.vector.tensor_copy(out=mem_grouped[:].bitcast(F32), in_=mem_bank[:].rearrange("p u m -> p m u"))
             nc.vector.quantize_mx(
                 out=mem_codes[:].bitcast(FP8X4),
                 scales=mem_scales[:],
@@ -59,12 +90,9 @@ def tile_gatedmemorymodule_pa_kernel(tc, queries, memory_items, out):
             )
 
             for c in range(CHUNKS):
-                raw = loads.tile([P, PACK, D], BF16)
-                nc.sync.dma_start(
-                    out=raw[:], in_=queries[c * PACK : (c + 1) * PACK].rearrange("t b d -> b t d")
-                )
+                raw = load_chunk(c)
 
-                q1_grouped = stage.tile([P, PACK, B, PACK], BF16, align_bytes=64)
+                q1_grouped = stage1.tile([P, PACK, B, PACK], BF16, align_bytes=64)
                 q1_words = q1_grouped[:].bitcast(F32)
                 for pair in range(PACK // 2):
                     bank = psum_t.tile([P, 2, HALVES, B], F32, tag="bank")
@@ -74,8 +102,11 @@ def tile_gatedmemorymodule_pa_kernel(tc, queries, memory_items, out):
                         out=q1_words[:, 2 * pair : 2 * pair + 2],
                         in_=bank[:].rearrange("p i u b -> p i b u"),
                     )
-                q1_codes = stage.tile([P, PACK * B], U32, align_bytes=64)
-                q1_scales = stage.tile([P, PACK * B], U8, align_bytes=64)
+                if c < SHARED:
+                    by_scalar = c % SCALAR_REGROUP_EVERY == SCALAR_REGROUP_EVERY - 1
+                    q2_grouped = regroup(raw, nc.scalar.copy if by_scalar else nc.vector.tensor_copy)
+                q1_codes = stage1.tile([P, PACK * B], U32, align_bytes=64)
+                q1_scales = stage1.tile([P, PACK * B], U8, align_bytes=64)
                 nc.vector.quantize_mx(
                     out=q1_codes[:].bitcast(FP8X4),
                     scales=q1_scales[:],
@@ -93,36 +124,30 @@ def tile_gatedmemorymodule_pa_kernel(tc, queries, memory_items, out):
                         stop=True,
                     )
                 nc.scalar.copy(out=scores[:, c], in_=score_bank[:].rearrange("p j m -> p m j"))
-                if c == 0:
-                    nc.vector.tensor_copy(out=running_max[:], in_=scores[:, c])
-                else:
+                if c < SHARED:
+                    quantise_q2(c, q2_grouped)
+                if c == 1:
+                    nc.vector.tensor_copy(out=running_max[:], in_=scores[:, 0:2])
+                elif c % 2 == 1:
                     nc.vector.tensor_tensor(
-                        out=running_max[:], in0=running_max[:], in1=scores[:, c], op=ALU.max
+                        out=running_max[:], in0=running_max[:], in1=scores[:, c - 1 : c + 1], op=ALU.max
                     )
 
-                q2_grouped = stage.tile([P, D, PACK], BF16, align_bytes=64)
-                dst = q2_grouped[:].rearrange("p (c i) t -> p c t i", i=4)
-                src = raw[:].rearrange("p t (c i) -> p c t i", i=4)
-                if c % SCALAR_REGROUP_EVERY == SCALAR_REGROUP_EVERY - 1:
-                    nc.scalar.copy(out=dst, in_=src)
-                else:
-                    nc.vector.tensor_copy(out=dst, in_=src)
-                nc.vector.quantize_mx(
-                    out=q2_codes[:, c, :].bitcast(FP8X4),
-                    scales=q2_scales[:, c, :],
-                    in_=q2_grouped[:].rearrange("p d t -> p (d t)"),
-                )
-
         with tc.tile_pool(name="soft", bufs=1) as soft:
+            at_the_barrier = [(c, regroup(load_chunk(c), nc.scalar.copy)) for c in range(SHARED, SHARED + AT_THE_BARRIER)]
             neg_max = soft.tile([P, M], F32)
-            nc.vector.tensor_reduce(out=neg_max[:], in_=running_max[:], axis=AXIS.X, op=ALU.max)
+            nc.vector.tensor_reduce(
+                out=neg_max[:], in_=running_max[:].rearrange("p k m j -> p m k j"), axis=AXIS.XY, op=ALU.max
+            )
             nc.vector.tensor_scalar_mul(out=neg_max[:], in0=neg_max[:], scalar1=-1.0 / TEMP)
+            for c, q2_grouped in at_the_barrier:
+                quantise_q2(c, q2_grouped)
             total = soft.tile([P, M], F32)
             inverse = soft.tile([P, M], F32)
             v_att = soft.tile([P, CHUNKS, M, PACK], BF16, align_bytes=64)
             v_codes = soft.tile([P, CHUNKS, M], U32, align_bytes=64)
             v_scales = soft.tile([P, CHUNKS, M], U8, align_bytes=64)
-            for g in range(M // SLOT_GROUP):
+            for g in range(GROUPS):
                 slots = slice(g * SLOT_GROUP, (g + 1) * SLOT_GROUP)
                 for m in range(g * SLOT_GROUP, (g + 1) * SLOT_GROUP):
                     nc.scalar.activation(
@@ -133,6 +158,8 @@ def tile_gatedmemorymodule_pa_kernel(tc, queries, memory_items, out):
                         scale=1.0 / TEMP,
                         accum_out=total[:, m : m + 1],
                     )
+                if g < BESIDE_EXP:
+                    q2_grouped = regroup(load_chunk(SHARED + AT_THE_BARRIER + g), nc.vector.tensor_copy)
                 nc.vector.reciprocal(out=inverse[:, slots], in_=total[:, slots])
                 nc.vector.tensor_tensor(
                     out=v_att[:, :, slots, :],
@@ -140,16 +167,19 @@ def tile_gatedmemorymodule_pa_kernel(tc, queries, memory_items, out):
                     in1=inverse[:, slots].unsqueeze(1).unsqueeze(3).to_broadcast([P, CHUNKS, SLOT_GROUP, PACK]),
                     op=ALU.mult,
                 )
+                if g < BESIDE_EXP:
+                    quantise_q2(SHARED + AT_THE_BARRIER + g, q2_grouped)
 
-            acc = psum_o.tile([P, D], F32)
-            wide = 8
-            for q in range(CHUNKS // wide):
-                part = slice(q * wide, (q + 1) * wide)
+            for q in range(CHUNKS // WIDE):
+                part = slice(q * WIDE, (q + 1) * WIDE)
                 nc.vector.quantize_mx(
                     out=v_codes[:, part, :].rearrange("p c m -> p (c m)").bitcast(FP8X4),
                     scales=v_scales[:, part, :].rearrange("p c m -> p (c m)"),
                     in_=v_att[:, part].rearrange("p c m t -> p (c m t)"),
                 )
+            for c in range(CHUNKS - AT_THE_END, CHUNKS):
+                quantise_q2(c, regroup(load_chunk(c), nc.scalar.copy))
+            acc = psum_o.tile([P, D], F32)
             for c in range(CHUNKS):
                 nc.tensor.matmul_mx(
                     out=acc[:],

@@ -19,6 +19,7 @@ HALVES = 2
 SLOT_GROUP = 16
 GROUPS = M // SLOT_GROUP
 WIDE = 8
+AHEAD = 3
 
 AT_THE_BARRIER = 1
 BESIDE_EXP = 3
@@ -37,11 +38,11 @@ def transpose_words(nc, bank, rows_bf16, ident):
 
 def tile_gatedmemorymodule_pa_kernel(tc, queries, memory_items, out):
     nc = tc.nc
-    with tc.tile_pool(name="keep", bufs=1) as keep, tc.tile_pool(name="loads", bufs=4) as loads, tc.tile_pool(
+    with tc.tile_pool(name="keep", bufs=1) as keep, tc.tile_pool(name="loads", bufs=AHEAD + 1) as loads, tc.tile_pool(
         name="stage2", bufs=3
     ) as stage2, tc.psum_pool(name="psum_t", bufs=4) as psum_t, tc.psum_pool(name="psum_s", bufs=2) as psum_s, tc.psum_pool(
         name="psum_o", bufs=1
-    ) as psum_o:
+    ) as psum_o, tc.manual_schedule():
         warm = keep.tile([P, 1], F32)
         nc.vector.memset(warm[:], 0.0)
         nc.scalar.activation(out=warm[:], in_=warm[:], func=ACT.Exp)
@@ -56,29 +57,89 @@ def tile_gatedmemorymodule_pa_kernel(tc, queries, memory_items, out):
         mem_scales = keep.tile([P, M], U8, align_bytes=64)
         running_max = keep.tile([P, 2, M, PACK], F32)
 
-        def load_chunk(c):
-            raw = loads.tile([P, PACK, D], BF16, name="raw")
-            nc.sync.dma_start(out=raw[:], in_=queries[c * PACK : (c + 1) * PACK].rearrange("t b d -> b t d"))
-            return raw
+        raw = {}
+        banks = {}
+        q1_grouped = {}
+        q1_packed = {}
+        score_bank = {}
+        q2_grouped = {}
 
-        def regroup(raw, copy):
-            q2_grouped = stage2.tile([P, D, PACK], BF16, align_bytes=64, name="q2_grouped")
+        def load(c):
+            raw[c] = loads.tile([P, PACK, D], BF16, name="raw")
+            nc.sync.dma_start(out=raw[c][:], in_=queries[c * PACK : (c + 1) * PACK].rearrange("t b d -> b t d"))
+
+        def regroup(c, copy):
+            q2_grouped[c] = stage2.tile([P, D, PACK], BF16, align_bytes=64, name="q2_grouped")
             copy(
-                out=q2_grouped[:].rearrange("p (c i) t -> p c t i", i=4),
-                in_=raw[:].rearrange("p t (c i) -> p c t i", i=4),
+                out=q2_grouped[c][:].rearrange("p (c i) t -> p c t i", i=4),
+                in_=raw[c][:].rearrange("p t (c i) -> p c t i", i=4),
             )
-            return q2_grouped
 
-        def quantise_q2(c, q2_grouped):
+        def quantise_q2(c):
             nc.vector.quantize_mx(
                 out=q2_codes[:, c, :].bitcast(FP8X4),
                 scales=q2_scales[:, c, :],
-                in_=q2_grouped[:].rearrange("p d t -> p (d t)"),
+                in_=q2_grouped[c][:].rearrange("p d t -> p (d t)"),
             )
 
         with tc.tile_pool(name="stage1", bufs=3) as stage1:
+
+            def transposes(c):
+                banks[c] = []
+                for pair in range(PACK // 2):
+                    bank = psum_t.tile([P, 2, HALVES, B], F32, tag="bank", name="bank")
+                    for i in range(2):
+                        transpose_words(nc, bank[:, i], raw[c][:, 2 * pair + i, :], ident)
+                    banks[c].append(bank)
+
+            def copy_out(c):
+                q1_grouped[c] = stage1.tile([P, PACK, B, PACK], BF16, align_bytes=64, name="q1_grouped")
+                q1_words = q1_grouped[c][:].bitcast(F32)
+                for pair in range(PACK // 2):
+                    nc.scalar.copy(
+                        out=q1_words[:, 2 * pair : 2 * pair + 2],
+                        in_=banks[c][pair][:].rearrange("p i u b -> p i b u"),
+                    )
+
+            def quantise_q1(c):
+                codes = stage1.tile([P, PACK * B], U32, align_bytes=64, name="q1_codes")
+                scales = stage1.tile([P, PACK * B], U8, align_bytes=64, name="q1_scales")
+                nc.vector.quantize_mx(
+                    out=codes[:].bitcast(FP8X4),
+                    scales=scales[:],
+                    in_=q1_grouped[c][:].rearrange("p t b k -> p (t b k)"),
+                )
+                q1_packed[c] = (codes, scales)
+
+            def first_product(c):
+                codes, scales = q1_packed[c]
+                score_bank[c] = psum_s.tile([P, PACK, M], F32, name="score_bank")
+                for j in range(PACK):
+                    nc.tensor.matmul_mx(
+                        out=score_bank[c][:, j, :],
+                        lhsT=codes[:, j * B : (j + 1) * B].bitcast(FP8X4),
+                        lhsT_scale=scales[:, j * B : (j + 1) * B],
+                        rhs=mem_codes[:].bitcast(FP8X4),
+                        rhs_scale=mem_scales[:],
+                        start=True,
+                        stop=True,
+                    )
+
+            def keep_scores(c):
+                nc.scalar.copy(out=scores[:, c], in_=score_bank[c][:].rearrange("p j m -> p m j"))
+
+            def maximum(c):
+                if c == 1:
+                    nc.vector.tensor_copy(out=running_max[:], in_=scores[:, 0:2])
+                else:
+                    nc.vector.tensor_tensor(
+                        out=running_max[:], in0=running_max[:], in1=scores[:, c - 1 : c + 1], op=ALU.max
+                    )
+
             mem_raw = stage1.tile([P, D], BF16, bufs=1)
             nc.sync.dma_start(out=mem_raw[:], in_=memory_items)
+            for c in range(AHEAD):
+                load(c)
             mem_bank = psum_t.tile([P, HALVES, M], F32, tag="bank")
             transpose_words(nc, mem_bank, mem_raw[:], ident)
             mem_grouped = stage1.tile([P, M, PACK], BF16, align_bytes=64, bufs=1)
@@ -89,59 +150,47 @@ def tile_gatedmemorymodule_pa_kernel(tc, queries, memory_items, out):
                 in_=mem_grouped[:].rearrange("p m k -> p (m k)"),
             )
 
-            for c in range(CHUNKS):
-                raw = load_chunk(c)
+            transposes(0)
+            for i in range(CHUNKS + 3):
+                if i + AHEAD < CHUNKS:
+                    load(i + AHEAD)
+                if i + 1 < CHUNKS:
+                    transposes(i + 1)
+                if i < CHUNKS:
+                    copy_out(i)
+                if 0 <= i - 1 < CHUNKS:
+                    quantise_q1(i - 1)
+                    first_product(i - 1)
+                if i < SHARED:
+                    by_scalar = i % SCALAR_REGROUP_EVERY == SCALAR_REGROUP_EVERY - 1
+                    regroup(i, nc.scalar.copy if by_scalar else nc.vector.tensor_copy)
+                if 0 <= i - 2 < CHUNKS:
+                    keep_scores(i - 2)
+                if 0 <= i - 3 < CHUNKS and (i - 3) % 2 == 1:
+                    maximum(i - 3)
+                if 0 <= i - 1 < SHARED:
+                    quantise_q2(i - 1)
 
-                q1_grouped = stage1.tile([P, PACK, B, PACK], BF16, align_bytes=64)
-                q1_words = q1_grouped[:].bitcast(F32)
-                for pair in range(PACK // 2):
-                    bank = psum_t.tile([P, 2, HALVES, B], F32, tag="bank")
-                    for i in range(2):
-                        transpose_words(nc, bank[:, i], raw[:, 2 * pair + i, :], ident)
-                    nc.scalar.copy(
-                        out=q1_words[:, 2 * pair : 2 * pair + 2],
-                        in_=bank[:].rearrange("p i u b -> p i b u"),
-                    )
-                if c < SHARED:
-                    by_scalar = c % SCALAR_REGROUP_EVERY == SCALAR_REGROUP_EVERY - 1
-                    q2_grouped = regroup(raw, nc.scalar.copy if by_scalar else nc.vector.tensor_copy)
-                q1_codes = stage1.tile([P, PACK * B], U32, align_bytes=64)
-                q1_scales = stage1.tile([P, PACK * B], U8, align_bytes=64)
-                nc.vector.quantize_mx(
-                    out=q1_codes[:].bitcast(FP8X4),
-                    scales=q1_scales[:],
-                    in_=q1_grouped[:].rearrange("p t b k -> p (t b k)"),
-                )
-                score_bank = psum_s.tile([P, PACK, M], F32)
-                for j in range(PACK):
-                    nc.tensor.matmul_mx(
-                        out=score_bank[:, j, :],
-                        lhsT=q1_codes[:, j * B : (j + 1) * B].bitcast(FP8X4),
-                        lhsT_scale=q1_scales[:, j * B : (j + 1) * B],
-                        rhs=mem_codes[:].bitcast(FP8X4),
-                        rhs_scale=mem_scales[:],
-                        start=True,
-                        stop=True,
-                    )
-                nc.scalar.copy(out=scores[:, c], in_=score_bank[:].rearrange("p j m -> p m j"))
-                if c < SHARED:
-                    quantise_q2(c, q2_grouped)
-                if c == 1:
-                    nc.vector.tensor_copy(out=running_max[:], in_=scores[:, 0:2])
-                elif c % 2 == 1:
-                    nc.vector.tensor_tensor(
-                        out=running_max[:], in0=running_max[:], in1=scores[:, c - 1 : c + 1], op=ALU.max
-                    )
+        late = list(range(SHARED, CHUNKS))
+
+        def regroup_late(n, copy):
+            regroup(late[n], copy)
+            if n + AHEAD < len(late):
+                load(late[n + AHEAD])
+
+        for c in late[:AHEAD]:
+            load(c)
 
         with tc.tile_pool(name="soft", bufs=1) as soft:
-            at_the_barrier = [(c, regroup(load_chunk(c), nc.scalar.copy)) for c in range(SHARED, SHARED + AT_THE_BARRIER)]
+            for n in range(AT_THE_BARRIER):
+                regroup_late(n, nc.scalar.copy)
             neg_max = soft.tile([P, M], F32)
             nc.vector.tensor_reduce(
                 out=neg_max[:], in_=running_max[:].rearrange("p k m j -> p m k j"), axis=AXIS.XY, op=ALU.max
             )
             nc.vector.tensor_scalar_mul(out=neg_max[:], in0=neg_max[:], scalar1=-1.0 / TEMP)
-            for c, q2_grouped in at_the_barrier:
-                quantise_q2(c, q2_grouped)
+            for n in range(AT_THE_BARRIER):
+                quantise_q2(late[n])
             total = soft.tile([P, M], F32)
             inverse = soft.tile([P, M], F32)
             v_att = soft.tile([P, CHUNKS, M, PACK], BF16, align_bytes=64)
@@ -159,7 +208,7 @@ def tile_gatedmemorymodule_pa_kernel(tc, queries, memory_items, out):
                         accum_out=total[:, m : m + 1],
                     )
                 if g < BESIDE_EXP:
-                    q2_grouped = regroup(load_chunk(SHARED + AT_THE_BARRIER + g), nc.vector.tensor_copy)
+                    regroup_late(AT_THE_BARRIER + g, nc.vector.tensor_copy)
                 nc.vector.reciprocal(out=inverse[:, slots], in_=total[:, slots])
                 nc.vector.tensor_tensor(
                     out=v_att[:, :, slots, :],
@@ -168,8 +217,10 @@ def tile_gatedmemorymodule_pa_kernel(tc, queries, memory_items, out):
                     op=ALU.mult,
                 )
                 if g < BESIDE_EXP:
-                    quantise_q2(SHARED + AT_THE_BARRIER + g, q2_grouped)
+                    quantise_q2(late[AT_THE_BARRIER + g])
 
+            for n in range(AT_THE_BARRIER + BESIDE_EXP, len(late)):
+                regroup_late(n, nc.scalar.copy)
             for q in range(CHUNKS // WIDE):
                 part = slice(q * WIDE, (q + 1) * WIDE)
                 nc.vector.quantize_mx(
@@ -177,8 +228,8 @@ def tile_gatedmemorymodule_pa_kernel(tc, queries, memory_items, out):
                     scales=v_scales[:, part, :].rearrange("p c m -> p (c m)"),
                     in_=v_att[:, part].rearrange("p c m t -> p (c m t)"),
                 )
-            for c in range(CHUNKS - AT_THE_END, CHUNKS):
-                quantise_q2(c, regroup(load_chunk(c), nc.scalar.copy))
+            for n in range(AT_THE_BARRIER + BESIDE_EXP, len(late)):
+                quantise_q2(late[n])
             acc = psum_o.tile([P, D], F32)
             for c in range(CHUNKS):
                 nc.tensor.matmul_mx(

@@ -22,10 +22,12 @@ WIDE = 8
 AHEAD = 3
 
 AT_THE_BARRIER = 1
-BESIDE_EXP = 3
-AT_THE_END = 6
+BESIDE_EXP = 5
+AT_THE_END = 5
 SHARED = CHUNKS - AT_THE_BARRIER - BESIDE_EXP - AT_THE_END
-SCALAR_REGROUP_EVERY = 3
+VECTOR_COLUMNS = slice(0, 320)
+SCALAR_COLUMNS = slice(320, D)
+ALL_COLUMNS = slice(0, D)
 
 FLOPS = 2 * 2 * T * B * D * M
 
@@ -68,11 +70,12 @@ def tile_gatedmemorymodule_pa_kernel(tc, queries, memory_items, out):
             raw[c] = loads.tile([P, PACK, D], BF16, name="raw")
             nc.sync.dma_start(out=raw[c][:], in_=queries[c * PACK : (c + 1) * PACK].rearrange("t b d -> b t d"))
 
-        def regroup(c, copy):
-            q2_grouped[c] = stage2.tile([P, D, PACK], BF16, align_bytes=64, name="q2_grouped")
+        def regroup(c, copy, columns):
+            if c not in q2_grouped:
+                q2_grouped[c] = stage2.tile([P, D, PACK], BF16, align_bytes=64, name="q2_grouped")
             copy(
-                out=q2_grouped[c][:].rearrange("p (c i) t -> p c t i", i=4),
-                in_=raw[c][:].rearrange("p t (c i) -> p c t i", i=4),
+                out=q2_grouped[c][:, columns, :].rearrange("p (c i) t -> p c t i", i=4),
+                in_=raw[c][:, :, columns].rearrange("p t (c i) -> p c t i", i=4),
             )
 
         def quantise_q2(c):
@@ -162,8 +165,8 @@ def tile_gatedmemorymodule_pa_kernel(tc, queries, memory_items, out):
                     quantise_q1(i - 1)
                     first_product(i - 1)
                 if i < SHARED:
-                    by_scalar = i % SCALAR_REGROUP_EVERY == SCALAR_REGROUP_EVERY - 1
-                    regroup(i, nc.scalar.copy if by_scalar else nc.vector.tensor_copy)
+                    regroup(i, nc.vector.tensor_copy, VECTOR_COLUMNS)
+                    regroup(i, nc.scalar.copy, SCALAR_COLUMNS)
                 if 0 <= i - 2 < CHUNKS:
                     keep_scores(i - 2)
                 if 0 <= i - 3 < CHUNKS and (i - 3) % 2 == 1:
@@ -174,7 +177,7 @@ def tile_gatedmemorymodule_pa_kernel(tc, queries, memory_items, out):
         late = list(range(SHARED, CHUNKS))
 
         def regroup_late(n, copy):
-            regroup(late[n], copy)
+            regroup(late[n], copy, ALL_COLUMNS)
             if n + AHEAD < len(late):
                 load(late[n + AHEAD])
 
@@ -196,6 +199,24 @@ def tile_gatedmemorymodule_pa_kernel(tc, queries, memory_items, out):
             v_att = soft.tile([P, CHUNKS, M, PACK], BF16, align_bytes=64)
             v_codes = soft.tile([P, CHUNKS, M], U32, align_bytes=64)
             v_scales = soft.tile([P, CHUNKS, M], U8, align_bytes=64)
+
+            def normalise(slots, first, count):
+                part = slice(first, first + count)
+                nc.vector.tensor_tensor(
+                    out=v_att[:, part, slots, :],
+                    in0=scores[:, part, slots, :],
+                    in1=inverse[:, slots].unsqueeze(1).unsqueeze(3).to_broadcast([P, count, SLOT_GROUP, PACK]),
+                    op=ALU.mult,
+                )
+
+            def quantise_v(first):
+                part = slice(first, first + WIDE)
+                nc.vector.quantize_mx(
+                    out=v_codes[:, part, :].rearrange("p c m -> p (c m)").bitcast(FP8X4),
+                    scales=v_scales[:, part, :].rearrange("p c m -> p (c m)"),
+                    in_=v_att[:, part].rearrange("p c m t -> p (c m t)"),
+                )
+
             for g in range(GROUPS):
                 slots = slice(g * SLOT_GROUP, (g + 1) * SLOT_GROUP)
                 for m in range(g * SLOT_GROUP, (g + 1) * SLOT_GROUP):
@@ -210,24 +231,18 @@ def tile_gatedmemorymodule_pa_kernel(tc, queries, memory_items, out):
                 if g < BESIDE_EXP:
                     regroup_late(AT_THE_BARRIER + g, nc.vector.tensor_copy)
                 nc.vector.reciprocal(out=inverse[:, slots], in_=total[:, slots])
-                nc.vector.tensor_tensor(
-                    out=v_att[:, :, slots, :],
-                    in0=scores[:, :, slots, :],
-                    in1=inverse[:, slots].unsqueeze(1).unsqueeze(3).to_broadcast([P, CHUNKS, SLOT_GROUP, PACK]),
-                    op=ALU.mult,
-                )
+                if g < GROUPS - 1:
+                    normalise(slots, 0, CHUNKS)
                 if g < BESIDE_EXP:
                     quantise_q2(late[AT_THE_BARRIER + g])
 
             for n in range(AT_THE_BARRIER + BESIDE_EXP, len(late)):
                 regroup_late(n, nc.scalar.copy)
-            for q in range(CHUNKS // WIDE):
-                part = slice(q * WIDE, (q + 1) * WIDE)
-                nc.vector.quantize_mx(
-                    out=v_codes[:, part, :].rearrange("p c m -> p (c m)").bitcast(FP8X4),
-                    scales=v_scales[:, part, :].rearrange("p c m -> p (c m)"),
-                    in_=v_att[:, part].rearrange("p c m t -> p (c m t)"),
-                )
+            for first in range(0, CHUNKS, WIDE):
+                normalise(slots, first, WIDE)
+                if first > 0:
+                    quantise_v(first - WIDE)
+            quantise_v(CHUNKS - WIDE)
             for n in range(AT_THE_BARRIER + BESIDE_EXP, len(late)):
                 quantise_q2(late[n])
             acc = psum_o.tile([P, D], F32)

@@ -22,11 +22,11 @@ WIDE = 8
 AHEAD = 3
 
 AT_THE_BARRIER = 1
-BESIDE_EXP = 5
+BESIDE_EXP = 2
 AT_THE_END = 5
 SHARED = CHUNKS - AT_THE_BARRIER - BESIDE_EXP - AT_THE_END
-VECTOR_COLUMNS = slice(0, 320)
-SCALAR_COLUMNS = slice(320, D)
+VECTOR_COLUMNS = slice(0, 352)
+SCALAR_COLUMNS = slice(352, D)
 ALL_COLUMNS = slice(0, D)
 
 FLOPS = 2 * 2 * T * B * D * M

@@ -16,20 +16,24 @@ T, B, D, M = 128, 128, 512, 128
 TEMP = 0.1
 CHUNKS = T // PACK
 HALVES = 2
-SLOT_GROUP = 16
-GROUPS = M // SLOT_GROUP
+ROUNDS = CHUNKS // 2
+AHEAD = 2
 WIDE = 8
-AHEAD = 3
+SLOT_GROUPS = [16, 16, 16, 16, 16, 16, 16, 8, 8]
 
-AT_THE_BARRIER = 1
-BESIDE_EXP = 2
-AT_THE_END = 5
-SHARED = CHUNKS - AT_THE_BARRIER - BESIDE_EXP - AT_THE_END
-VECTOR_COLUMNS = slice(0, 352)
-SCALAR_COLUMNS = slice(352, D)
+TURN = 6
+LATE = [c for c in range(CHUNKS) if c % TURN in (4, 5)]
+LATE_ON_VECTOR = 4
+THIRDS = [slice(0, 176), slice(176, 352), slice(352, 512)]
 ALL_COLUMNS = slice(0, D)
 
 FLOPS = 2 * 2 * T * B * D * M
+
+
+def round_chunks(r):
+    turn, step = divmod(r, 3)
+    first, second = ((0, 1), (2, 4), (3, 5))[step]
+    return turn * TURN + first, turn * TURN + second
 
 
 def transpose_words(nc, bank, rows_bf16, ident):
@@ -40,9 +44,9 @@ def transpose_words(nc, bank, rows_bf16, ident):
 
 def tile_gatedmemorymodule_pa_kernel(tc, queries, memory_items, out):
     nc = tc.nc
-    with tc.tile_pool(name="keep", bufs=1) as keep, tc.tile_pool(name="loads", bufs=AHEAD + 1) as loads, tc.tile_pool(
-        name="stage2", bufs=3
-    ) as stage2, tc.psum_pool(name="psum_t", bufs=4) as psum_t, tc.psum_pool(name="psum_s", bufs=2) as psum_s, tc.psum_pool(
+    with tc.tile_pool(name="keep", bufs=1) as keep, tc.tile_pool(name="late_loads", bufs=4) as late_loads, tc.tile_pool(
+        name="stage2", bufs=2
+    ) as stage2, tc.psum_pool(name="psum_t", bufs=4) as psum_t, tc.psum_pool(name="psum_s", bufs=3) as psum_s, tc.psum_pool(
         name="psum_o", bufs=1
     ) as psum_o, tc.manual_schedule():
         warm = keep.tile([P, 1], F32)
@@ -51,41 +55,51 @@ def tile_gatedmemorymodule_pa_kernel(tc, queries, memory_items, out):
 
         ident = keep.tile([P, P], F32)
         make_identity(nc, ident[:])
+        ident_bf16 = keep.tile([P, P], BF16)
+        make_identity(nc, ident_bf16[:])
 
         scores = keep.tile([P, CHUNKS, M, PACK], F32)
         q2_codes = keep.tile([P, CHUNKS, D], U32, align_bytes=64)
         q2_scales = keep.tile([P, CHUNKS, D], U8, align_bytes=64)
         mem_codes = keep.tile([P, M], U32, align_bytes=64)
         mem_scales = keep.tile([P, M], U8, align_bytes=64)
-        running_max = keep.tile([P, 2, M, PACK], F32)
+        round_max = keep.tile([P, M, PACK], BF16)
+        running_max = keep.tile([P, M, PACK], BF16)
 
         raw = {}
-        banks = {}
-        q1_grouped = {}
-        q1_packed = {}
-        score_bank = {}
         q2_grouped = {}
 
-        def load(c):
-            raw[c] = loads.tile([P, PACK, D], BF16, name="raw")
-            nc.sync.dma_start(out=raw[c][:], in_=queries[c * PACK : (c + 1) * PACK].rearrange("t b d -> b t d"))
+        def load(c, pool, pieces=1, tag="raw", bufs=None):
+            raw[c] = pool.tile([P, PACK, D], BF16, name="raw", tag=tag, bufs=bufs)
+            steps = PACK // pieces
+            for i in range(0, PACK, steps):
+                nc.sync.dma_start(
+                    out=raw[c][:, i : i + steps],
+                    in_=queries[c * PACK + i : c * PACK + i + steps].rearrange("t b d -> b t d"),
+                )
+
+        def grouped(c):
+            if c - c % 2 not in q2_grouped:
+                q2_grouped[c - c % 2] = stage2.tile([P, 2, D, PACK], BF16, align_bytes=64, name="q2_grouped")
+            return q2_grouped[c - c % 2][:, c % 2]
 
         def regroup(c, copy, columns):
-            if c not in q2_grouped:
-                q2_grouped[c] = stage2.tile([P, D, PACK], BF16, align_bytes=64, name="q2_grouped")
             copy(
-                out=q2_grouped[c][:, columns, :].rearrange("p (c i) t -> p c t i", i=4),
+                out=grouped(c)[:, columns, :].rearrange("p (c i) t -> p c t i", i=4),
                 in_=raw[c][:, :, columns].rearrange("p t (c i) -> p c t i", i=4),
             )
 
         def quantise_q2(c):
             nc.vector.quantize_mx(
-                out=q2_codes[:, c, :].bitcast(FP8X4),
-                scales=q2_scales[:, c, :],
-                in_=q2_grouped[c][:].rearrange("p d t -> p (d t)"),
+                out=q2_codes[:, c : c + 2, :].rearrange("p c d -> p (c d)").bitcast(FP8X4),
+                scales=q2_scales[:, c : c + 2, :].rearrange("p c d -> p (c d)"),
+                in_=q2_grouped[c][:].rearrange("p c d t -> p (c d t)"),
             )
 
-        with tc.tile_pool(name="stage1", bufs=3) as stage1:
+        with tc.tile_pool(name="loads", bufs=5) as loads, tc.tile_pool(name="stage1", bufs=2) as stage1:
+            banks = {}
+            q1_grouped = {}
+            score_bank = {}
 
             def transposes(c):
                 banks[c] = []
@@ -95,55 +109,73 @@ def tile_gatedmemorymodule_pa_kernel(tc, queries, memory_items, out):
                         transpose_words(nc, bank[:, i], raw[c][:, 2 * pair + i, :], ident)
                     banks[c].append(bank)
 
-            def copy_out(c):
-                q1_grouped[c] = stage1.tile([P, PACK, B, PACK], BF16, align_bytes=64, name="q1_grouped")
-                q1_words = q1_grouped[c][:].bitcast(F32)
+            def copy_out(r, half):
+                if half == 0:
+                    q1_grouped[r] = stage1.tile([P, 2, PACK, B, PACK], BF16, align_bytes=64, name="q1_grouped")
+                q1_words = q1_grouped[r][:, half].bitcast(F32)
                 for pair in range(PACK // 2):
                     nc.scalar.copy(
                         out=q1_words[:, 2 * pair : 2 * pair + 2],
-                        in_=banks[c][pair][:].rearrange("p i u b -> p i b u"),
+                        in_=banks[round_chunks(r)[half]][pair][:].rearrange("p i u b -> p i b u"),
                     )
 
-            def quantise_q1(c):
-                codes = stage1.tile([P, PACK * B], U32, align_bytes=64, name="q1_codes")
-                scales = stage1.tile([P, PACK * B], U8, align_bytes=64, name="q1_scales")
+            def first_product(r):
+                codes = stage1.tile([P, 2, PACK * B], U32, align_bytes=64, name="q1_codes")
+                scales = stage1.tile([P, 2, PACK * B], U8, align_bytes=64, name="q1_scales")
                 nc.vector.quantize_mx(
-                    out=codes[:].bitcast(FP8X4),
-                    scales=scales[:],
-                    in_=q1_grouped[c][:].rearrange("p t b k -> p (t b k)"),
+                    out=codes[:].rearrange("p c r -> p (c r)").bitcast(FP8X4),
+                    scales=scales[:].rearrange("p c r -> p (c r)"),
+                    in_=q1_grouped[r][:].rearrange("p c t b k -> p (c t b k)"),
                 )
-                q1_packed[c] = (codes, scales)
-
-            def first_product(c):
-                codes, scales = q1_packed[c]
-                score_bank[c] = psum_s.tile([P, PACK, M], F32, name="score_bank")
-                for j in range(PACK):
-                    nc.tensor.matmul_mx(
-                        out=score_bank[c][:, j, :],
-                        lhsT=codes[:, j * B : (j + 1) * B].bitcast(FP8X4),
-                        lhsT_scale=scales[:, j * B : (j + 1) * B],
-                        rhs=mem_codes[:].bitcast(FP8X4),
-                        rhs_scale=mem_scales[:],
-                        start=True,
-                        stop=True,
-                    )
+                for half in range(2):
+                    bank = psum_s.tile([P, PACK, M], F32, name="score_bank")
+                    score_bank[round_chunks(r)[half]] = bank
+                    for j in range(PACK):
+                        nc.tensor.matmul_mx(
+                            out=bank[:, j, :],
+                            lhsT=codes[:, half, j * B : (j + 1) * B].bitcast(FP8X4),
+                            lhsT_scale=scales[:, half, j * B : (j + 1) * B],
+                            rhs=mem_codes[:].bitcast(FP8X4),
+                            rhs_scale=mem_scales[:],
+                            start=True,
+                            stop=True,
+                        )
 
             def keep_scores(c):
                 nc.scalar.copy(out=scores[:, c], in_=score_bank[c][:].rearrange("p j m -> p m j"))
 
-            def maximum(c):
-                if c == 1:
-                    nc.vector.tensor_copy(out=running_max[:], in_=scores[:, 0:2])
-                else:
-                    nc.vector.tensor_tensor(
-                        out=running_max[:], in0=running_max[:], in1=scores[:, c - 1 : c + 1], op=ALU.max
-                    )
+            def maximum_of_round(r):
+                first, second = round_chunks(r)
+                nc.vector.tensor_tensor(
+                    out=running_max[:] if r == 0 else round_max[:],
+                    in0=scores[:, first],
+                    in1=scores[:, second],
+                    op=ALU.max,
+                )
 
+            def take_in_maximum(r):
+                if r > 0:
+                    nc.vector.tensor_tensor(out=running_max[:], in0=running_max[:], in1=round_max[:], op=ALU.max)
+
+            def load_round(r):
+                for c in round_chunks(r):
+                    if c % TURN == 1:
+                        load(c, loads, tag="raw_scalar", bufs=2)
+                    else:
+                        load(c, loads, tag="raw", bufs=5)
+
+            def scalars_third(step):
+                turn, third = divmod(step, 3)
+                regroup(turn * TURN + 1, nc.scalar.copy, THIRDS[third])
+
+            load(0, loads, pieces=2, tag="raw", bufs=5)
             mem_raw = stage1.tile([P, D], BF16, bufs=1)
             nc.sync.dma_start(out=mem_raw[:], in_=memory_items)
-            for c in range(AHEAD):
-                load(c)
-            mem_bank = psum_t.tile([P, HALVES, M], F32, tag="bank")
+            load(1, loads, tag="raw_scalar", bufs=2)
+            for r in range(1, AHEAD):
+                load_round(r)
+            transposes(round_chunks(0)[0])
+            mem_bank = psum_s.tile([P, HALVES, M], F32, name="mem_bank", tag="score_bank")
             transpose_words(nc, mem_bank, mem_raw[:], ident)
             mem_grouped = stage1.tile([P, M, PACK], BF16, align_bytes=64, bufs=1)
             nc.vector.tensor_copy(out=mem_grouped[:].bitcast(F32), in_=mem_bank[:].rearrange("p u m -> p m u"))
@@ -153,47 +185,44 @@ def tile_gatedmemorymodule_pa_kernel(tc, queries, memory_items, out):
                 in_=mem_grouped[:].rearrange("p m k -> p (m k)"),
             )
 
-            transposes(0)
-            for i in range(CHUNKS + 3):
-                if i + AHEAD < CHUNKS:
-                    load(i + AHEAD)
-                if i + 1 < CHUNKS:
-                    transposes(i + 1)
-                if i < CHUNKS:
-                    copy_out(i)
-                if 0 <= i - 1 < CHUNKS:
-                    quantise_q1(i - 1)
-                    first_product(i - 1)
-                if i < SHARED:
-                    regroup(i, nc.vector.tensor_copy, VECTOR_COLUMNS)
-                    regroup(i, nc.scalar.copy, SCALAR_COLUMNS)
-                if 0 <= i - 2 < CHUNKS:
-                    keep_scores(i - 2)
-                if 0 <= i - 3 < CHUNKS and (i - 3) % 2 == 1:
-                    maximum(i - 3)
-                if 0 <= i - 1 < SHARED:
-                    quantise_q2(i - 1)
-
-        late = list(range(SHARED, CHUNKS))
-
-        def regroup_late(n, copy):
-            regroup(late[n], copy, ALL_COLUMNS)
-            if n + AHEAD < len(late):
-                load(late[n + AHEAD])
-
-        for c in late[:AHEAD]:
-            load(c)
+            for r in range(ROUNDS + 2):
+                if r + AHEAD < ROUNDS:
+                    load_round(r + AHEAD)
+                if r == ROUNDS - AHEAD:
+                    for c in LATE[:4]:
+                        load(c, late_loads, tag="raw_late", bufs=4)
+                if r < ROUNDS:
+                    transposes(round_chunks(r)[1])
+                    copy_out(r, 0)
+                if r < ROUNDS:
+                    copy_out(r, 1)
+                if 1 <= r <= ROUNDS:
+                    first_product(r - 1)
+                if r + 1 < ROUNDS:
+                    transposes(round_chunks(r + 1)[0])
+                if r >= 2:
+                    maximum_of_round(r - 2)
+                if 3 <= r <= ROUNDS and r % 3 == 0:
+                    quantise_q2((r // 3 - 1) * TURN)
+                if 4 <= r and r % 3 == 1:
+                    quantise_q2((r // 3 - 1) * TURN + 2)
+                if r < ROUNDS:
+                    regroup(round_chunks(r)[0], nc.vector.tensor_copy, ALL_COLUMNS)
+                if r >= ROUNDS:
+                    scalars_third(r)
+                if 1 <= r <= ROUNDS:
+                    for c in round_chunks(r - 1):
+                        keep_scores(c)
+                if r < ROUNDS:
+                    scalars_third(r)
+                if r >= 2:
+                    take_in_maximum(r - 2)
 
         with tc.tile_pool(name="soft", bufs=1) as soft:
-            for n in range(AT_THE_BARRIER):
-                regroup_late(n, nc.scalar.copy)
             neg_max = soft.tile([P, M], F32)
-            nc.vector.tensor_reduce(
-                out=neg_max[:], in_=running_max[:].rearrange("p k m j -> p m k j"), axis=AXIS.XY, op=ALU.max
-            )
+            nc.vector.tensor_reduce(out=neg_max[:], in_=running_max[:], axis=AXIS.X, op=ALU.max)
             nc.vector.tensor_scalar_mul(out=neg_max[:], in0=neg_max[:], scalar1=-1.0 / TEMP)
-            for n in range(AT_THE_BARRIER):
-                quantise_q2(late[n])
+            quantise_q2(CHUNKS - 2)
             total = soft.tile([P, M], F32)
             inverse = soft.tile([P, M], F32)
             v_att = soft.tile([P, CHUNKS, M, PACK], BF16, align_bytes=64)
@@ -205,7 +234,7 @@ def tile_gatedmemorymodule_pa_kernel(tc, queries, memory_items, out):
                 nc.vector.tensor_tensor(
                     out=v_att[:, part, slots, :],
                     in0=scores[:, part, slots, :],
-                    in1=inverse[:, slots].unsqueeze(1).unsqueeze(3).to_broadcast([P, count, SLOT_GROUP, PACK]),
+                    in1=inverse[:, slots].unsqueeze(1).unsqueeze(3).to_broadcast([P, count, slots.stop - slots.start, PACK]),
                     op=ALU.mult,
                 )
 
@@ -217,9 +246,46 @@ def tile_gatedmemorymodule_pa_kernel(tc, queries, memory_items, out):
                     in_=v_att[:, part].rearrange("p c m t -> p (c m t)"),
                 )
 
-            for g in range(GROUPS):
-                slots = slice(g * SLOT_GROUP, (g + 1) * SLOT_GROUP)
-                for m in range(g * SLOT_GROUP, (g + 1) * SLOT_GROUP):
+            def vector_late(g):
+                if g == 0:
+                    regroup(LATE[0], nc.vector.tensor_copy, ALL_COLUMNS)
+                    regroup(LATE[1], nc.vector.tensor_copy, ALL_COLUMNS)
+                if g == 1:
+                    quantise_q2(LATE[0])
+                if g == 2 or g == 3:
+                    regroup(LATE[g], nc.vector.tensor_copy, ALL_COLUMNS)
+                if g == 4:
+                    quantise_q2(LATE[2])
+
+            id_banks = {}
+
+            def interleave_on_tensor(c):
+                id_banks[c] = []
+                for half in range(2):
+                    bank = psum_t.tile([P, 2, D], BF16, tag="bank", name="id_bank")
+                    for i in range(2):
+                        first = (2 * half + i) * P
+                        nc.tensor.matmul(
+                            out=bank[:, i, :],
+                            lhsT=ident_bf16[:],
+                            rhs=raw[c][:, :, first : first + P].rearrange("p t d -> p d t"),
+                            start=True,
+                            stop=True,
+                        )
+                    id_banks[c].append(bank)
+
+            def take_interleaved(c):
+                for half in range(2):
+                    nc.scalar.copy(
+                        out=grouped(c)[:, 256 * half : 256 * half + 256, :].rearrange("p d t -> p (d t)"),
+                        in_=id_banks[c][half][:].rearrange("p i n -> p (i n)"),
+                    )
+
+            first_slot = 0
+            for g, count in enumerate(SLOT_GROUPS):
+                slots = slice(first_slot, first_slot + count)
+                first_slot += count
+                for m in range(slots.start, slots.stop):
                     nc.scalar.activation(
                         out=scores[:, :, m, :],
                         in_=scores[:, :, m, :],
@@ -228,34 +294,55 @@ def tile_gatedmemorymodule_pa_kernel(tc, queries, memory_items, out):
                         scale=1.0 / TEMP,
                         accum_out=total[:, m : m + 1],
                     )
-                if g < BESIDE_EXP:
-                    regroup_late(AT_THE_BARRIER + g, nc.vector.tensor_copy)
+                vector_late(g)
+                if g == 0:
+                    for c in LATE[4:6]:
+                        load(c, late_loads, tag="raw_late", bufs=4)
+                if g == 3:
+                    for c in LATE[6:8]:
+                        load(c, late_loads, tag="raw_late", bufs=4)
+                if g == 4:
+                    for c in LATE[4:6]:
+                        interleave_on_tensor(c)
+                    for c in LATE[8:10]:
+                        load(c, late_loads, tag="raw_late", bufs=4)
                 nc.vector.reciprocal(out=inverse[:, slots], in_=total[:, slots])
-                if g < GROUPS - 1:
+                if g < len(SLOT_GROUPS) - 1:
                     normalise(slots, 0, CHUNKS)
-                if g < BESIDE_EXP:
-                    quantise_q2(late[AT_THE_BARRIER + g])
 
-            for n in range(AT_THE_BARRIER + BESIDE_EXP, len(late)):
-                regroup_late(n, nc.scalar.copy)
-            for first in range(0, CHUNKS, WIDE):
-                normalise(slots, first, WIDE)
-                if first > 0:
-                    quantise_v(first - WIDE)
-            quantise_v(CHUNKS - WIDE)
-            for n in range(AT_THE_BARRIER + BESIDE_EXP, len(late)):
-                quantise_q2(late[n])
             acc = psum_o.tile([P, D], F32)
-            for c in range(CHUNKS):
+            on_tensor = LATE[LATE_ON_VECTOR:]
+
+            def second_product(c, start, stop):
                 nc.tensor.matmul_mx(
                     out=acc[:],
                     lhsT=v_codes[:, c, :].bitcast(FP8X4),
                     lhsT_scale=v_scales[:, c, :],
                     rhs=q2_codes[:, c, :].bitcast(FP8X4),
                     rhs_scale=q2_scales[:, c, :],
-                    start=(c == 0),
-                    stop=(c == CHUNKS - 1),
+                    start=start,
+                    stop=stop,
                 )
+
+            for n in range(0, len(on_tensor), 2):
+                pair = on_tensor[n : n + 2]
+                for c in pair:
+                    take_interleaved(c)
+                for c in on_tensor[n + 2 : n + 4]:
+                    interleave_on_tensor(c)
+                normalise(slots, n * WIDE // 2, WIDE)
+                if n > 0:
+                    quantise_v((n // 2 - 1) * WIDE)
+                    quantise_q2(on_tensor[n - 2])
+            normalise(slots, 3 * WIDE, WIDE)
+            quantise_v(2 * WIDE)
+            quantise_q2(on_tensor[-2])
+            quantise_v(3 * WIDE)
+            ready = [c for c in range(CHUNKS) if c not in on_tensor]
+            for c in ready:
+                second_product(c, start=(c == ready[0]), stop=False)
+            for c in on_tensor:
+                second_product(c, start=False, stop=(c == on_tensor[-1]))
             result = soft.tile([P, D], F32)
             nc.scalar.mul(out=result[:], in_=acc[:], mul=1.0 / B)
             nc.sync.dma_start(out=out, in_=result[:])

@@ -55,8 +55,6 @@ def tile_gatedmemorymodule_pa_kernel(tc, queries, memory_items, out):
 
         ident = keep.tile([P, P], F32)
         make_identity(nc, ident[:])
-        ident_bf16 = keep.tile([P, P], BF16)
-        make_identity(nc, ident_bf16[:])
 
         scores = keep.tile([P, CHUNKS, M, PACK], F32)
         q2_codes = keep.tile([P, CHUNKS, D], U32, align_bytes=64)
@@ -257,30 +255,6 @@ def tile_gatedmemorymodule_pa_kernel(tc, queries, memory_items, out):
                 if g == 4:
                     quantise_q2(LATE[2])
 
-            id_banks = {}
-
-            def interleave_on_tensor(c):
-                id_banks[c] = []
-                for half in range(2):
-                    bank = psum_t.tile([P, 2, D], BF16, tag="bank", name="id_bank")
-                    for i in range(2):
-                        first = (2 * half + i) * P
-                        nc.tensor.matmul(
-                            out=bank[:, i, :],
-                            lhsT=ident_bf16[:],
-                            rhs=raw[c][:, :, first : first + P].rearrange("p t d -> p d t"),
-                            start=True,
-                            stop=True,
-                        )
-                    id_banks[c].append(bank)
-
-            def take_interleaved(c):
-                for half in range(2):
-                    nc.scalar.copy(
-                        out=grouped(c)[:, 256 * half : 256 * half + 256, :].rearrange("p d t -> p (d t)"),
-                        in_=id_banks[c][half][:].rearrange("p i n -> p (i n)"),
-                    )
-
             first_slot = 0
             for g, count in enumerate(SLOT_GROUPS):
                 slots = slice(first_slot, first_slot + count)
@@ -301,17 +275,12 @@ def tile_gatedmemorymodule_pa_kernel(tc, queries, memory_items, out):
                 if g == 3:
                     for c in LATE[6:8]:
                         load(c, late_loads, tag="raw_late", bufs=4)
-                if g == 4:
-                    for c in LATE[4:6]:
-                        interleave_on_tensor(c)
-                    for c in LATE[8:10]:
-                        load(c, late_loads, tag="raw_late", bufs=4)
                 nc.vector.reciprocal(out=inverse[:, slots], in_=total[:, slots])
                 if g < len(SLOT_GROUPS) - 1:
                     normalise(slots, 0, CHUNKS)
 
             acc = psum_o.tile([P, D], F32)
-            on_tensor = LATE[LATE_ON_VECTOR:]
+            at_the_end = LATE[LATE_ON_VECTOR:]
 
             def second_product(c, start, stop):
                 nc.tensor.matmul_mx(
@@ -324,25 +293,26 @@ def tile_gatedmemorymodule_pa_kernel(tc, queries, memory_items, out):
                     stop=stop,
                 )
 
-            for n in range(0, len(on_tensor), 2):
-                pair = on_tensor[n : n + 2]
+            for n in range(0, len(at_the_end), 2):
+                pair = at_the_end[n : n + 2]
                 for c in pair:
-                    take_interleaved(c)
-                for c in on_tensor[n + 2 : n + 4]:
-                    interleave_on_tensor(c)
+                    regroup(c, nc.scalar.copy, ALL_COLUMNS)
+                if n == 0:
+                    for c in at_the_end[4:6]:
+                        load(c, late_loads, tag="raw_late", bufs=4)
                 normalise(slots, n * WIDE // 2, WIDE)
                 if n > 0:
                     quantise_v((n // 2 - 1) * WIDE)
-                    quantise_q2(on_tensor[n - 2])
+                    quantise_q2(at_the_end[n - 2])
             normalise(slots, 3 * WIDE, WIDE)
             quantise_v(2 * WIDE)
-            quantise_q2(on_tensor[-2])
+            quantise_q2(at_the_end[-2])
             quantise_v(3 * WIDE)
-            ready = [c for c in range(CHUNKS) if c not in on_tensor]
+            ready = [c for c in range(CHUNKS) if c not in at_the_end]
             for c in ready:
                 second_product(c, start=(c == ready[0]), stop=False)
-            for c in on_tensor:
-                second_product(c, start=False, stop=(c == on_tensor[-1]))
+            for c in at_the_end:
+                second_product(c, start=False, stop=(c == at_the_end[-1]))
             result = soft.tile([P, D], F32)
             nc.scalar.mul(out=result[:], in_=acc[:], mul=1.0 / B)
             nc.sync.dma_start(out=out, in_=result[:])

@@ -23,7 +23,7 @@ SLOT_GROUPS = [16, 16, 16, 16, 16, 16, 16, 8, 8]
 
 TURN = 6
 LATE = [c for c in range(CHUNKS) if c % TURN in (4, 5)]
-LATE_ON_VECTOR = 4
+AT_THE_BARRIER, BESIDE_EXP, AFTER_EXP, AT_THE_END = LATE[0:2], LATE[2:4], LATE[4:8], LATE[8:10]
 THIRDS = [slice(0, 176), slice(176, 352), slice(352, 512)]
 ALL_COLUMNS = slice(0, D)
 
@@ -55,6 +55,8 @@ def tile_gatedmemorymodule_pa_kernel(tc, queries, memory_items, out):
 
         ident = keep.tile([P, P], F32)
         make_identity(nc, ident[:])
+        ident_bf16 = keep.tile([P, P], BF16)
+        make_identity(nc, ident_bf16[:])
 
         scores = keep.tile([P, CHUNKS, M, PACK], F32)
         q2_codes = keep.tile([P, CHUNKS, D], U32, align_bytes=64)
@@ -66,6 +68,7 @@ def tile_gatedmemorymodule_pa_kernel(tc, queries, memory_items, out):
 
         raw = {}
         q2_grouped = {}
+        interleaved = {}
 
         def load(c, pool, pieces=1, tag="raw", bufs=None):
             raw[c] = pool.tile([P, PACK, D], BF16, name="raw", tag=tag, bufs=bufs)
@@ -92,6 +95,25 @@ def tile_gatedmemorymodule_pa_kernel(tc, queries, memory_items, out):
                 out=q2_codes[:, c : c + 2, :].rearrange("p c d -> p (c d)").bitcast(FP8X4),
                 scales=q2_scales[:, c : c + 2, :].rearrange("p c d -> p (c d)"),
                 in_=q2_grouped[c][:].rearrange("p c d t -> p (c d t)"),
+            )
+
+        def interleave_on_tensor(c, half, pool, tag):
+            bank = pool.tile([P, D // 2, PACK], BF16, tag=tag, name="interleaved")
+            columns = slice(half * D // 2, (half + 1) * D // 2)
+            for t in range(0, PACK, 2):
+                nc.tensor.matmul(
+                    out=bank[:, :, t : t + 2],
+                    lhsT=ident_bf16[:],
+                    rhs=raw[c][:, t : t + 2, columns].rearrange("p t d -> p d t"),
+                    start=True,
+                    stop=True,
+                )
+            interleaved[c, half] = bank
+
+        def take_interleaved(c, half):
+            nc.scalar.copy(
+                out=grouped(c)[:, half * D // 2 : (half + 1) * D // 2, :],
+                in_=interleaved[c, half][:],
             )
 
         with tc.tile_pool(name="loads", bufs=5) as loads, tc.tile_pool(name="stage1", bufs=2) as stage1:
@@ -187,7 +209,7 @@ def tile_gatedmemorymodule_pa_kernel(tc, queries, memory_items, out):
                 if r + AHEAD < ROUNDS:
                     load_round(r + AHEAD)
                 if r == ROUNDS - AHEAD:
-                    for c in LATE[:4]:
+                    for c in AT_THE_BARRIER + BESIDE_EXP:
                         load(c, late_loads, tag="raw_late", bufs=4)
                 if r < ROUNDS:
                     transposes(round_chunks(r)[1])
@@ -215,6 +237,9 @@ def tile_gatedmemorymodule_pa_kernel(tc, queries, memory_items, out):
                     scalars_third(r)
                 if r >= 2:
                     take_in_maximum(r - 2)
+
+        for c in AT_THE_BARRIER:
+            regroup(c, nc.scalar.copy, ALL_COLUMNS)
 
         with tc.tile_pool(name="soft", bufs=1) as soft:
             neg_max = soft.tile([P, M], F32)
@@ -246,15 +271,16 @@ def tile_gatedmemorymodule_pa_kernel(tc, queries, memory_items, out):
 
             def vector_late(g):
                 if g == 0:
-                    regroup(LATE[0], nc.vector.tensor_copy, ALL_COLUMNS)
-                    regroup(LATE[1], nc.vector.tensor_copy, ALL_COLUMNS)
+                    for c in BESIDE_EXP:
+                        regroup(c, nc.vector.tensor_copy, ALL_COLUMNS)
                 if g == 1:
-                    quantise_q2(LATE[0])
-                if g == 2 or g == 3:
-                    regroup(LATE[g], nc.vector.tensor_copy, ALL_COLUMNS)
+                    quantise_q2(AT_THE_BARRIER[0])
+                if g == 2:
+                    quantise_q2(BESIDE_EXP[0])
                 if g == 4:
-                    quantise_q2(LATE[2])
+                    regroup(AT_THE_END[0], nc.vector.tensor_copy, ALL_COLUMNS)
 
+            after_exp = [(c, half) for c in AFTER_EXP for half in range(2)]
             first_slot = 0
             for g, count in enumerate(SLOT_GROUPS):
                 slots = slice(first_slot, first_slot + count)
@@ -270,17 +296,21 @@ def tile_gatedmemorymodule_pa_kernel(tc, queries, memory_items, out):
                     )
                 vector_late(g)
                 if g == 0:
-                    for c in LATE[4:6]:
+                    for c in (AT_THE_END[0], *AFTER_EXP[0:2], AT_THE_END[1]):
                         load(c, late_loads, tag="raw_late", bufs=4)
-                if g == 3:
-                    for c in LATE[6:8]:
-                        load(c, late_loads, tag="raw_late", bufs=4)
+                if g == 4:
+                    for n, (c, half) in enumerate(after_exp[:4]):
+                        interleave_on_tensor(c, half, psum_t, "bank")
+                if g == 5:
+                    load(AFTER_EXP[2], late_loads, tag="raw_late", bufs=4)
+                    load(AFTER_EXP[3], late_loads, tag="raw_late", bufs=4)
+                    for n, (c, half) in enumerate(after_exp[4:7]):
+                        interleave_on_tensor(c, half, psum_s, "score_bank")
                 nc.vector.reciprocal(out=inverse[:, slots], in_=total[:, slots])
                 if g < len(SLOT_GROUPS) - 1:
                     normalise(slots, 0, CHUNKS)
 
             acc = psum_o.tile([P, D], F32)
-            at_the_end = LATE[LATE_ON_VECTOR:]
 
             def second_product(c, start, stop):
                 nc.tensor.matmul_mx(
@@ -293,26 +323,27 @@ def tile_gatedmemorymodule_pa_kernel(tc, queries, memory_items, out):
                     stop=stop,
                 )
 
-            for n in range(0, len(at_the_end), 2):
-                pair = at_the_end[n : n + 2]
-                for c in pair:
-                    regroup(c, nc.scalar.copy, ALL_COLUMNS)
-                if n == 0:
-                    for c in at_the_end[4:6]:
-                        load(c, late_loads, tag="raw_late", bufs=4)
-                normalise(slots, n * WIDE // 2, WIDE)
-                if n > 0:
-                    quantise_v((n // 2 - 1) * WIDE)
-                    quantise_q2(at_the_end[n - 2])
+            regroup(AT_THE_END[1], nc.scalar.copy, ALL_COLUMNS)
+            for c, half in after_exp[:4]:
+                take_interleaved(c, half)
+            interleave_on_tensor(*after_exp[7], psum_t, "bank")
+            normalise(slots, 0, WIDE)
+            normalise(slots, WIDE, WIDE)
+            quantise_v(0)
+            normalise(slots, 2 * WIDE, WIDE)
+            quantise_q2(AT_THE_END[0])
+            for c, half in after_exp[4:]:
+                take_interleaved(c, half)
+            quantise_v(WIDE)
             normalise(slots, 3 * WIDE, WIDE)
+            quantise_q2(AFTER_EXP[0])
             quantise_v(2 * WIDE)
-            quantise_q2(at_the_end[-2])
             quantise_v(3 * WIDE)
-            ready = [c for c in range(CHUNKS) if c not in at_the_end]
-            for c in ready:
-                second_product(c, start=(c == ready[0]), stop=False)
-            for c in at_the_end:
-                second_product(c, start=False, stop=(c == at_the_end[-1]))
+            quantise_q2(AFTER_EXP[2])
+            last = AT_THE_END + AFTER_EXP
+            order = [c for c in range(CHUNKS) if c not in last] + last
+            for c in order:
+                second_product(c, start=(c == order[0]), stop=(c == order[-1]))
             result = soft.tile([P, D], F32)
             nc.scalar.mul(out=result[:], in_=acc[:], mul=1.0 / B)
             nc.sync.dma_start(out=out, in_=result[:])

@@ -46,9 +46,7 @@ def tile_gatedmemorymodule_pa_kernel(tc, queries, memory_items, out):
     nc = tc.nc
     with tc.tile_pool(name="keep", bufs=1) as keep, tc.tile_pool(name="late_loads", bufs=4) as late_loads, tc.tile_pool(
         name="stage2", bufs=2
-    ) as stage2, tc.psum_pool(name="psum_t", bufs=4) as psum_t, tc.psum_pool(name="psum_s", bufs=3) as psum_s, tc.psum_pool(
-        name="psum_o", bufs=1
-    ) as psum_o, tc.manual_schedule():
+    ) as stage2, tc.psum_pool(name="psum_t", bufs=4) as psum_t, tc.psum_pool(name="psum_s", bufs=4) as psum_s, tc.manual_schedule():
         warm = keep.tile([P, 1], F32)
         nc.vector.memset(warm[:], 0.0)
         nc.scalar.activation(out=warm[:], in_=warm[:], func=ACT.Exp)
@@ -214,29 +212,32 @@ def tile_gatedmemorymodule_pa_kernel(tc, queries, memory_items, out):
                 if r < ROUNDS:
                     transposes(round_chunks(r)[1])
                     copy_out(r, 0)
-                if r < ROUNDS:
-                    copy_out(r, 1)
-                if 1 <= r <= ROUNDS:
-                    first_product(r - 1)
                 if r + 1 < ROUNDS:
                     transposes(round_chunks(r + 1)[0])
-                if r >= 2:
-                    maximum_of_round(r - 2)
+                if 2 <= r <= ROUNDS:
+                    keep_scores(round_chunks(r - 2)[0])
+                if r < ROUNDS:
+                    copy_out(r, 1)
+                if 2 <= r <= ROUNDS:
+                    keep_scores(round_chunks(r - 2)[1])
+                if 1 <= r <= ROUNDS:
+                    first_product(r - 1)
+                scalars_third(r)
+                if r == ROUNDS:
+                    for c in round_chunks(r - 1):
+                        keep_scores(c)
+                if 3 <= r:
+                    maximum_of_round(r - 3)
                 if 3 <= r <= ROUNDS and r % 3 == 0:
                     quantise_q2((r // 3 - 1) * TURN)
                 if 4 <= r and r % 3 == 1:
                     quantise_q2((r // 3 - 1) * TURN + 2)
                 if r < ROUNDS:
                     regroup(round_chunks(r)[0], nc.vector.tensor_copy, ALL_COLUMNS)
-                if r >= ROUNDS:
-                    scalars_third(r)
-                if 1 <= r <= ROUNDS:
-                    for c in round_chunks(r - 1):
-                        keep_scores(c)
-                if r < ROUNDS:
-                    scalars_third(r)
-                if r >= 2:
-                    take_in_maximum(r - 2)
+                if 3 <= r:
+                    take_in_maximum(r - 3)
+            maximum_of_round(ROUNDS - 1)
+            take_in_maximum(ROUNDS - 1)
 
         for c in AT_THE_BARRIER:
             regroup(c, nc.scalar.copy, ALL_COLUMNS)
@@ -310,7 +311,7 @@ def tile_gatedmemorymodule_pa_kernel(tc, queries, memory_items, out):
                 if g < len(SLOT_GROUPS) - 1:
                     normalise(slots, 0, CHUNKS)
 
-            acc = psum_o.tile([P, D], F32)
+            acc = psum_s.tile([P, D], F32, tag="score_bank", name="acc")
 
             def second_product(c, start, stop):
                 nc.tensor.matmul_mx(

@@ -19,7 +19,7 @@ HALVES = 2
 ROUNDS = CHUNKS // 2
 AHEAD = 2
 WIDE = 8
-SLOT_GROUPS = [16, 16, 16, 16, 16, 16, 16, 8, 8]
+SLOT_GROUPS = [16, 32, 32, 24, 16, 8]
 
 TURN = 6
 LATE = [c for c in range(CHUNKS) if c % TURN in (4, 5)]
@@ -61,8 +61,8 @@ def tile_gatedmemorymodule_pa_kernel(tc, queries, memory_items, out):
         q2_scales = keep.tile([P, CHUNKS, D], U8, align_bytes=64)
         mem_codes = keep.tile([P, M], U32, align_bytes=64)
         mem_scales = keep.tile([P, M], U8, align_bytes=64)
-        round_max = keep.tile([P, M, PACK], BF16)
-        running_max = keep.tile([P, M, PACK], BF16)
+        turn_min = keep.tile([P, 3, M, PACK], BF16)
+        running_min = keep.tile([P, 3, M, PACK], BF16)
 
         raw = {}
         q2_grouped = {}
@@ -160,20 +160,14 @@ def tile_gatedmemorymodule_pa_kernel(tc, queries, memory_items, out):
                         )
 
             def keep_scores(c):
-                nc.scalar.copy(out=scores[:, c], in_=score_bank[c][:].rearrange("p j m -> p m j"))
+                nc.scalar.mul(out=scores[:, c], in_=score_bank[c][:].rearrange("p j m -> p m j"), mul=-1.0 / TEMP)
 
-            def maximum_of_round(r):
-                first, second = round_chunks(r)
-                nc.vector.tensor_tensor(
-                    out=running_max[:] if r == 0 else round_max[:],
-                    in0=scores[:, first],
-                    in1=scores[:, second],
-                    op=ALU.max,
-                )
+            def minimum(out, in0, in1):
+                nc.vector.tensor_tensor(out=out, in0=in0, in1=in1, op=ALU.min)
 
-            def take_in_maximum(r):
-                if r > 0:
-                    nc.vector.tensor_tensor(out=running_max[:], in0=running_max[:], in1=round_max[:], op=ALU.max)
+            def minimum_of_turn(turn):
+                c = turn * TURN
+                minimum((turn_min if turn else running_min)[:], scores[:, c : c + 3], scores[:, c + 3 : c + 6])
 
             def load_round(r):
                 for c in round_chunks(r):
@@ -184,7 +178,7 @@ def tile_gatedmemorymodule_pa_kernel(tc, queries, memory_items, out):
 
             def scalars_third(step):
                 turn, third = divmod(step, 3)
-                regroup(turn * TURN + 1, nc.scalar.copy, THIRDS[third])
+                regroup(turn * TURN + 1, nc.scalar.copy if turn else nc.vector.tensor_copy, THIRDS[third])
 
             load(0, loads, pieces=2, tag="raw", bufs=5)
             mem_raw = stage1.tile([P, D], BF16, bufs=1)
@@ -193,6 +187,7 @@ def tile_gatedmemorymodule_pa_kernel(tc, queries, memory_items, out):
             for r in range(1, AHEAD):
                 load_round(r)
             transposes(round_chunks(0)[0])
+            regroup(round_chunks(0)[0], nc.vector.tensor_copy, ALL_COLUMNS)
             mem_bank = psum_s.tile([P, HALVES, M], F32, name="mem_bank", tag="score_bank")
             transpose_words(nc, mem_bank, mem_raw[:], ident)
             mem_grouped = stage1.tile([P, M, PACK], BF16, align_bytes=64, bufs=1)
@@ -222,30 +217,34 @@ def tile_gatedmemorymodule_pa_kernel(tc, queries, memory_items, out):
                     keep_scores(round_chunks(r - 2)[1])
                 if 1 <= r <= ROUNDS:
                     first_product(r - 1)
-                scalars_third(r)
-                if r == ROUNDS:
-                    for c in round_chunks(r - 1):
-                        keep_scores(c)
-                if 3 <= r:
-                    maximum_of_round(r - 3)
+                if 5 <= r < ROUNDS and r % 3 == 2:
+                    minimum_of_turn(r // 3 - 1)
                 if 3 <= r <= ROUNDS and r % 3 == 0:
                     quantise_q2((r // 3 - 1) * TURN)
                 if 4 <= r and r % 3 == 1:
                     quantise_q2((r // 3 - 1) * TURN + 2)
-                if r < ROUNDS:
+                if r == ROUNDS:
+                    minimum_of_turn(r // 3 - 1)
+                scalars_third(r)
+                if r == ROUNDS:
+                    for c in round_chunks(r - 1):
+                        keep_scores(c)
+                if 0 < r < ROUNDS:
                     regroup(round_chunks(r)[0], nc.vector.tensor_copy, ALL_COLUMNS)
-                if 3 <= r:
-                    take_in_maximum(r - 3)
-            maximum_of_round(ROUNDS - 1)
-            take_in_maximum(ROUNDS - 1)
+                if 8 < r <= ROUNDS and r % 3 == 0:
+                    minimum(running_min[:], running_min[:], turn_min[:])
+            minimum(running_min[:], running_min[:], turn_min[:])
+            minimum(running_min[:, 0], running_min[:, 0], running_min[:, 1])
+            minimum(turn_min[:, 0], scores[:, CHUNKS - 2], scores[:, CHUNKS - 1])
+            minimum(running_min[:, 0], running_min[:, 0], running_min[:, 2])
+            minimum(running_min[:, 0], running_min[:, 0], turn_min[:, 0])
 
         for c in AT_THE_BARRIER:
             regroup(c, nc.scalar.copy, ALL_COLUMNS)
 
         with tc.tile_pool(name="soft", bufs=1) as soft:
             neg_max = soft.tile([P, M], F32)
-            nc.vector.tensor_reduce(out=neg_max[:], in_=running_max[:], axis=AXIS.X, op=ALU.max)
-            nc.vector.tensor_scalar_mul(out=neg_max[:], in0=neg_max[:], scalar1=-1.0 / TEMP)
+            nc.vector.tensor_reduce(out=neg_max[:], in_=running_min[:, 0], axis=AXIS.X, op=ALU.min)
             quantise_q2(CHUNKS - 2)
             total = soft.tile([P, M], F32)
             inverse = soft.tile([P, M], F32)
@@ -274,12 +273,14 @@ def tile_gatedmemorymodule_pa_kernel(tc, queries, memory_items, out):
                 if g == 0:
                     for c in BESIDE_EXP:
                         regroup(c, nc.vector.tensor_copy, ALL_COLUMNS)
-                if g == 1:
                     quantise_q2(AT_THE_BARRIER[0])
-                if g == 2:
                     quantise_q2(BESIDE_EXP[0])
-                if g == 4:
+                if g == 1:
                     regroup(AT_THE_END[0], nc.vector.tensor_copy, ALL_COLUMNS)
+                if g == 2:
+                    regroup(AT_THE_END[1], nc.vector.tensor_copy, ALL_COLUMNS)
+                if g == 3:
+                    quantise_q2(AT_THE_END[0])
 
             after_exp = [(c, half) for c in AFTER_EXP for half in range(2)]
             first_slot = 0
@@ -292,21 +293,24 @@ def tile_gatedmemorymodule_pa_kernel(tc, queries, memory_items, out):
                         in_=scores[:, :, m, :],
                         func=ACT.Exp,
                         bias=neg_max[:, m : m + 1],
-                        scale=1.0 / TEMP,
+                        scale=-1.0,
                         accum_out=total[:, m : m + 1],
                     )
                 vector_late(g)
                 if g == 0:
                     for c in (AT_THE_END[0], *AFTER_EXP[0:2], AT_THE_END[1]):
                         load(c, late_loads, tag="raw_late", bufs=4)
-                if g == 4:
-                    for n, (c, half) in enumerate(after_exp[:4]):
+                if g == 1:
+                    for c, half in after_exp[:4]:
                         interleave_on_tensor(c, half, psum_t, "bank")
-                if g == 5:
-                    load(AFTER_EXP[2], late_loads, tag="raw_late", bufs=4)
-                    load(AFTER_EXP[3], late_loads, tag="raw_late", bufs=4)
-                    for n, (c, half) in enumerate(after_exp[4:7]):
+                    for c in AFTER_EXP[2:4]:
+                        load(c, late_loads, tag="raw_late", bufs=4)
+                if g == 2:
+                    for c, half in after_exp[4:7]:
                         interleave_on_tensor(c, half, psum_s, "score_bank")
+                if g == 3:
+                    take_interleaved(*after_exp[0])
+                    interleave_on_tensor(*after_exp[7], psum_t, "bank")
                 nc.vector.reciprocal(out=inverse[:, slots], in_=total[:, slots])
                 if g < len(SLOT_GROUPS) - 1:
                     normalise(slots, 0, CHUNKS)
@@ -324,24 +328,21 @@ def tile_gatedmemorymodule_pa_kernel(tc, queries, memory_items, out):
                     stop=stop,
                 )
 
-            regroup(AT_THE_END[1], nc.scalar.copy, ALL_COLUMNS)
-            for c, half in after_exp[:4]:
+            for c, half in after_exp[1:4]:
                 take_interleaved(c, half)
-            interleave_on_tensor(*after_exp[7], psum_t, "bank")
             normalise(slots, 0, WIDE)
             normalise(slots, WIDE, WIDE)
             quantise_v(0)
             normalise(slots, 2 * WIDE, WIDE)
-            quantise_q2(AT_THE_END[0])
-            for c, half in after_exp[4:]:
-                take_interleaved(c, half)
             quantise_v(WIDE)
             normalise(slots, 3 * WIDE, WIDE)
+            for c, half in after_exp[4:]:
+                take_interleaved(c, half)
             quantise_q2(AFTER_EXP[0])
             quantise_v(2 * WIDE)
             quantise_v(3 * WIDE)
             quantise_q2(AFTER_EXP[2])
-            last = AT_THE_END + AFTER_EXP
+            last = AFTER_EXP
             order = [c for c in range(CHUNKS) if c not in last] + last
             for c in order:
                 second_product(c, start=(c == order[0]), stop=(c == order[-1]))

@@ -18,6 +18,7 @@ CHUNKS = T // PACK
 HALVES = 2
 ROUNDS = CHUNKS // 2
 AHEAD = 2
+WARM_UPS = 4
 WIDE = 8
 SLOT_GROUPS = [16, 32, 32, 24, 16, 8]
 
@@ -261,8 +262,8 @@ def tile_gatedmemorymodule_pa_kernel(tc, queries, memory_items, out):
                     op=ALU.mult,
                 )
 
-            def quantise_v(first):
-                part = slice(first, first + WIDE)
+            def quantise_v(first, count):
+                part = slice(first, first + count)
                 nc.vector.quantize_mx(
                     out=v_codes[:, part, :].rearrange("p c m -> p (c m)").bitcast(FP8X4),
                     scales=v_scales[:, part, :].rearrange("p c m -> p (c m)"),
@@ -308,7 +309,7 @@ def tile_gatedmemorymodule_pa_kernel(tc, queries, memory_items, out):
                 if g == 2:
                     for c, half in after_exp[4:7]:
                         interleave_on_tensor(c, half, psum_s, "score_bank")
-                if g == 3:
+                if g == len(SLOT_GROUPS) - 1:
                     take_interleaved(*after_exp[0])
                     interleave_on_tensor(*after_exp[7], psum_t, "bank")
                 nc.vector.reciprocal(out=inverse[:, slots], in_=total[:, slots])
@@ -316,6 +317,8 @@ def tile_gatedmemorymodule_pa_kernel(tc, queries, memory_items, out):
                     normalise(slots, 0, CHUNKS)
 
             acc = psum_s.tile([P, D], F32, tag="score_bank", name="acc")
+            for n in range(WARM_UPS):
+                nc.tensor.matmul(out=acc[:, :M], lhsT=ident[:], rhs=inverse[:], start=True, stop=True)
 
             def second_product(c, start, stop):
                 nc.tensor.matmul_mx(
@@ -330,18 +333,17 @@ def tile_gatedmemorymodule_pa_kernel(tc, queries, memory_items, out):
 
             for c, half in after_exp[1:4]:
                 take_interleaved(c, half)
-            normalise(slots, 0, WIDE)
-            normalise(slots, WIDE, WIDE)
-            quantise_v(0)
-            normalise(slots, 2 * WIDE, WIDE)
-            quantise_v(WIDE)
-            normalise(slots, 3 * WIDE, WIDE)
             for c, half in after_exp[4:]:
                 take_interleaved(c, half)
-            quantise_q2(AFTER_EXP[0])
-            quantise_v(2 * WIDE)
-            quantise_v(3 * WIDE)
-            quantise_q2(AFTER_EXP[2])
+            normalise(slots, 0, WIDE)
+            normalise(slots, WIDE, WIDE)
+            quantise_v(0, WIDE // 2)
+            normalise(slots, 2 * WIDE, 2 * WIDE)
+            quantise_v(WIDE // 2, WIDE // 2)
+            for first in range(WIDE, CHUNKS, WIDE):
+                quantise_v(first, WIDE)
+            for c in AFTER_EXP[::2]:
+                quantise_q2(c)
             last = AFTER_EXP
             order = [c for c in range(CHUNKS) if c not in last] + last
             for c in order:

@@ -179,7 +179,8 @@ def tile_gatedmemorymodule_pa_kernel(tc, queries, memory_items, out):
 
             def scalars_third(step):
                 turn, third = divmod(step, 3)
-                regroup(turn * TURN + 1, nc.scalar.copy if turn else nc.vector.tensor_copy, THIRDS[third])
+                chunk = turn * TURN + (0 if turn == ROUNDS // 3 else 1)
+                regroup(chunk, nc.scalar.copy if turn else nc.vector.tensor_copy, THIRDS[third])
 
             load(0, loads, pieces=2, tag="raw", bufs=5)
             mem_raw = stage1.tile([P, D], BF16, bufs=1)
@@ -203,7 +204,7 @@ def tile_gatedmemorymodule_pa_kernel(tc, queries, memory_items, out):
                 if r + AHEAD < ROUNDS:
                     load_round(r + AHEAD)
                 if r == ROUNDS - AHEAD:
-                    for c in AT_THE_BARRIER + BESIDE_EXP:
+                    for c in AT_THE_BARRIER + BESIDE_EXP[:1]:
                         load(c, late_loads, tag="raw_late", bufs=4)
                 if r < ROUNDS:
                     transposes(round_chunks(r)[1])
@@ -230,7 +231,7 @@ def tile_gatedmemorymodule_pa_kernel(tc, queries, memory_items, out):
                 if r == ROUNDS:
                     for c in round_chunks(r - 1):
                         keep_scores(c)
-                if 0 < r < ROUNDS:
+                if 0 < r < ROUNDS - 1:
                     regroup(round_chunks(r)[0], nc.vector.tensor_copy, ALL_COLUMNS)
                 if 8 < r <= ROUNDS and r % 3 == 0:
                     minimum(running_min[:], running_min[:], turn_min[:])
@@ -240,13 +241,14 @@ def tile_gatedmemorymodule_pa_kernel(tc, queries, memory_items, out):
             minimum(running_min[:, 0], running_min[:, 0], running_min[:, 2])
             minimum(running_min[:, 0], running_min[:, 0], turn_min[:, 0])
 
+        load(CHUNKS - 1, late_loads, tag="raw_late", bufs=4)
         for c in AT_THE_BARRIER:
             regroup(c, nc.scalar.copy, ALL_COLUMNS)
+        load(BESIDE_EXP[1], late_loads, tag="raw_late", bufs=4)
 
         with tc.tile_pool(name="soft", bufs=1) as soft:
             neg_max = soft.tile([P, M], F32)
             nc.vector.tensor_reduce(out=neg_max[:], in_=running_min[:, 0], axis=AXIS.X, op=ALU.min)
-            quantise_q2(CHUNKS - 2)
             total = soft.tile([P, M], F32)
             inverse = soft.tile([P, M], F32)
             v_att = soft.tile([P, CHUNKS, M, PACK], BF16, align_bytes=64)
@@ -272,11 +274,13 @@ def tile_gatedmemorymodule_pa_kernel(tc, queries, memory_items, out):
 
             def vector_late(g):
                 if g == 0:
+                    regroup(CHUNKS - 1, nc.vector.tensor_copy, ALL_COLUMNS)
+                    quantise_q2(AT_THE_BARRIER[0])
+                    quantise_q2(CHUNKS - 2)
                     for c in BESIDE_EXP:
                         regroup(c, nc.vector.tensor_copy, ALL_COLUMNS)
-                    quantise_q2(AT_THE_BARRIER[0])
-                    quantise_q2(BESIDE_EXP[0])
                 if g == 1:
+                    quantise_q2(BESIDE_EXP[0])
                     regroup(AT_THE_END[0], nc.vector.tensor_copy, ALL_COLUMNS)
                 if g == 2:
                     regroup(AT_THE_END[1], nc.vector.tensor_copy, ALL_COLUMNS)

@@ -179,8 +179,9 @@ def tile_gatedmemorymodule_pa_kernel(tc, queries, memory_items, out):
 
             def scalars_third(step):
                 turn, third = divmod(step, 3)
-                chunk = turn * TURN + (0 if turn == ROUNDS // 3 else 1)
-                regroup(chunk, nc.scalar.copy if turn else nc.vector.tensor_copy, THIRDS[third])
+                if turn > 0:
+                    chunk = turn * TURN + (0 if turn == ROUNDS // 3 else 1)
+                    regroup(chunk, nc.scalar.copy, THIRDS[third])
 
             load(0, loads, pieces=2, tag="raw", bufs=5)
             mem_raw = stage1.tile([P, D], BF16, bufs=1)
@@ -231,6 +232,8 @@ def tile_gatedmemorymodule_pa_kernel(tc, queries, memory_items, out):
                 if r == ROUNDS:
                     for c in round_chunks(r - 1):
                         keep_scores(c)
+                if r == 0:
+                    regroup(round_chunks(r)[1], nc.vector.tensor_copy, ALL_COLUMNS)
                 if 0 < r < ROUNDS - 1:
                     regroup(round_chunks(r)[0], nc.vector.tensor_copy, ALL_COLUMNS)
                 if 8 < r <= ROUNDS and r % 3 == 0:
@@ -242,8 +245,8 @@ def tile_gatedmemorymodule_pa_kernel(tc, queries, memory_items, out):
             minimum(running_min[:, 0], running_min[:, 0], turn_min[:, 0])
 
         load(CHUNKS - 1, late_loads, tag="raw_late", bufs=4)
-        for c in AT_THE_BARRIER:
-            regroup(c, nc.scalar.copy, ALL_COLUMNS)
+        regroup(AT_THE_BARRIER[0], nc.scalar.copy, ALL_COLUMNS)
+        regroup(AT_THE_BARRIER[1], nc.scalar.copy, slice(0, D // 2))
         load(BESIDE_EXP[1], late_loads, tag="raw_late", bufs=4)
 
         with tc.tile_pool(name="soft", bufs=1) as soft:
@@ -275,10 +278,11 @@ def tile_gatedmemorymodule_pa_kernel(tc, queries, memory_items, out):
             def vector_late(g):
                 if g == 0:
                     regroup(CHUNKS - 1, nc.vector.tensor_copy, ALL_COLUMNS)
-                    quantise_q2(AT_THE_BARRIER[0])
+                    regroup(AT_THE_BARRIER[1], nc.vector.tensor_copy, slice(D // 2, D))
                     quantise_q2(CHUNKS - 2)
                     for c in BESIDE_EXP:
                         regroup(c, nc.vector.tensor_copy, ALL_COLUMNS)
+                    quantise_q2(AT_THE_BARRIER[0])
                 if g == 1:
                     quantise_q2(BESIDE_EXP[0])
                     regroup(AT_THE_END[0], nc.vector.tensor_copy, ALL_COLUMNS)
@@ -319,6 +323,12 @@ def tile_gatedmemorymodule_pa_kernel(tc, queries, memory_items, out):
                 nc.vector.reciprocal(out=inverse[:, slots], in_=total[:, slots])
                 if g < len(SLOT_GROUPS) - 1:
                     normalise(slots, 0, CHUNKS)
+
+            for m in range(M - 4, M):
+                nc.scalar.activation(
+                    out=v_att[:, :, m, :], in_=scores[:, :, m, :], func=ACT.Copy, scale=inverse[:, m : m + 1]
+                )
+            slots = slice(slots.start, M - 4)
 
             acc = psum_s.tile([P, D], F32, tag="score_bank", name="acc")
             for n in range(WARM_UPS):

@@ -62,8 +62,7 @@ def tile_gatedmemorymodule_pa_kernel(tc, queries, memory_items, out):
         q2_scales = keep.tile([P, CHUNKS, D], U8, align_bytes=64)
         mem_codes = keep.tile([P, M], U32, align_bytes=64)
         mem_scales = keep.tile([P, M], U8, align_bytes=64)
-        turn_min = keep.tile([P, 3, M, PACK], BF16)
-        running_min = keep.tile([P, 3, M, PACK], BF16)
+        neg_max = keep.tile([P, M], BF16)
 
         raw = {}
         q2_grouped = {}
@@ -77,6 +76,9 @@ def tile_gatedmemorymodule_pa_kernel(tc, queries, memory_items, out):
                     out=raw[c][:, i : i + steps],
                     in_=queries[c * PACK + i : c * PACK + i + steps].rearrange("t b d -> b t d"),
                 )
+
+        def load_late(c):
+            load(c, late_loads, tag="raw_late", bufs=4)
 
         def grouped(c):
             if c - c % 2 not in q2_grouped:
@@ -116,6 +118,8 @@ def tile_gatedmemorymodule_pa_kernel(tc, queries, memory_items, out):
             )
 
         with tc.tile_pool(name="loads", bufs=5) as loads, tc.tile_pool(name="stage1", bufs=2) as stage1:
+            turn_min = stage1.tile([P, 3, M, PACK], BF16, bufs=1)
+            running_min = stage1.tile([P, 3, M, PACK], BF16, bufs=1)
             banks = {}
             q1_grouped = {}
             score_bank = {}
@@ -184,7 +188,7 @@ def tile_gatedmemorymodule_pa_kernel(tc, queries, memory_items, out):
                     regroup(chunk, nc.scalar.copy, THIRDS[third])
 
             load(0, loads, pieces=2, tag="raw", bufs=5)
-            mem_raw = stage1.tile([P, D], BF16, bufs=1)
+            mem_raw = late_loads.tile([P, D], BF16, tag="raw_late", bufs=4, name="mem_raw")
             nc.sync.dma_start(out=mem_raw[:], in_=memory_items)
             load(1, loads, tag="raw_scalar", bufs=2)
             for r in range(1, AHEAD):
@@ -243,6 +247,7 @@ def tile_gatedmemorymodule_pa_kernel(tc, queries, memory_items, out):
             minimum(turn_min[:, 0], scores[:, CHUNKS - 2], scores[:, CHUNKS - 1])
             minimum(running_min[:, 0], running_min[:, 0], running_min[:, 2])
             minimum(running_min[:, 0], running_min[:, 0], turn_min[:, 0])
+            nc.vector.tensor_reduce(out=neg_max[:], in_=running_min[:, 0], axis=AXIS.X, op=ALU.min)
 
         load(CHUNKS - 1, late_loads, tag="raw_late", bufs=4)
         regroup(AT_THE_BARRIER[0], nc.scalar.copy, ALL_COLUMNS)
@@ -250,8 +255,7 @@ def tile_gatedmemorymodule_pa_kernel(tc, queries, memory_items, out):
         load(BESIDE_EXP[1], late_loads, tag="raw_late", bufs=4)
 
         with tc.tile_pool(name="soft", bufs=1) as soft:
-            neg_max = soft.tile([P, M], F32)
-            nc.vector.tensor_reduce(out=neg_max[:], in_=running_min[:, 0], axis=AXIS.X, op=ALU.min)
+            q2_grouped[AT_THE_END[0]] = soft.tile([P, 2, D, PACK], BF16, align_bytes=64, name="last_grouped")
             total = soft.tile([P, M], F32)
             inverse = soft.tile([P, M], F32)
             v_att = soft.tile([P, CHUNKS, M, PACK], BF16, align_bytes=64)
@@ -286,10 +290,6 @@ def tile_gatedmemorymodule_pa_kernel(tc, queries, memory_items, out):
                 if g == 1:
                     quantise_q2(BESIDE_EXP[0])
                     regroup(AT_THE_END[0], nc.vector.tensor_copy, ALL_COLUMNS)
-                if g == 2:
-                    regroup(AT_THE_END[1], nc.vector.tensor_copy, ALL_COLUMNS)
-                if g == 3:
-                    quantise_q2(AT_THE_END[0])
 
             after_exp = [(c, half) for c in AFTER_EXP for half in range(2)]
             first_slot = 0
@@ -324,15 +324,15 @@ def tile_gatedmemorymodule_pa_kernel(tc, queries, memory_items, out):
                 if g < len(SLOT_GROUPS) - 1:
                     normalise(slots, 0, CHUNKS)
 
-            for m in range(M - 4, M):
-                nc.scalar.activation(
-                    out=v_att[:, :, m, :], in_=scores[:, :, m, :], func=ACT.Copy, scale=inverse[:, m : m + 1]
-                )
-            slots = slice(slots.start, M - 4)
-
             acc = psum_s.tile([P, D], F32, tag="score_bank", name="acc")
             for n in range(WARM_UPS):
-                nc.tensor.matmul(out=acc[:, :M], lhsT=ident[:], rhs=inverse[:], start=True, stop=True)
+                nc.tensor.matmul(
+                    out=acc[:, : slots.start * PACK],
+                    lhsT=ident_bf16[:],
+                    rhs=v_att[:, 0, : slots.start, :].rearrange("p m t -> p (m t)"),
+                    start=True,
+                    stop=True,
+                )
 
             def second_product(c, start, stop):
                 nc.tensor.matmul_mx(
@@ -345,10 +345,9 @@ def tile_gatedmemorymodule_pa_kernel(tc, queries, memory_items, out):
                     stop=stop,
                 )
 
-            for c, half in after_exp[1:4]:
+            for c, half in after_exp[1:]:
                 take_interleaved(c, half)
-            for c, half in after_exp[4:]:
-                take_interleaved(c, half)
+            regroup(AT_THE_END[1], nc.scalar.copy, ALL_COLUMNS)
             normalise(slots, 0, WIDE)
             normalise(slots, WIDE, WIDE)
             quantise_v(0, WIDE // 2)
@@ -356,12 +355,12 @@ def tile_gatedmemorymodule_pa_kernel(tc, queries, memory_items, out):
             quantise_v(WIDE // 2, WIDE // 2)
             for first in range(WIDE, CHUNKS, WIDE):
                 quantise_v(first, WIDE)
-            for c in AFTER_EXP[::2]:
+            for c in (*AFTER_EXP[::2], AT_THE_END[0]):
                 quantise_q2(c)
-            last = AFTER_EXP
+            last = AFTER_EXP + AT_THE_END
             order = [c for c in range(CHUNKS) if c not in last] + last
             for c in order:
                 second_product(c, start=(c == order[0]), stop=(c == order[-1]))
-            result = soft.tile([P, D], F32)
+            result = late_loads.tile([P, D], F32, tag="raw_late", bufs=4, name="result")
             nc.scalar.mul(out=result[:], in_=acc[:], mul=1.0 / B)
             nc.sync.dma_start(out=out, in_=result[:])

import concourse.mybir as mybir
from concourse.masks import make_identity

F32 = mybir.dt.float32
BF16 = mybir.dt.bfloat16
U32 = mybir.dt.uint32
U8 = mybir.dt.uint8
FP8X4 = mybir.dt.float8_e4m3fn_x4
ALU = mybir.AluOpType
ACT = mybir.ActivationFunctionType
AXIS = mybir.AxisListType

P = 128
PACK = 4
T, B, D, M = 128, 128, 512, 128
TEMP = 0.1
CHUNKS = T // PACK
HALVES = 2
ROUNDS = CHUNKS // 2
AHEAD = 2
WARM_UPS = 4
WIDE = 8
SLOT_GROUPS = [16, 32, 32, 24, 16, 8]

TURN = 6
LATE = [c for c in range(CHUNKS) if c % TURN in (4, 5)]
AT_THE_BARRIER, BESIDE_EXP, AFTER_EXP, AT_THE_END = LATE[0:2], LATE[2:4], LATE[4:8], LATE[8:10]
THIRDS = [slice(0, 176), slice(176, 352), slice(352, 512)]
ALL_COLUMNS = slice(0, D)

FLOPS = 2 * 2 * T * B * D * M


def round_chunks(r):
    turn, step = divmod(r, 3)
    first, second = ((0, 1), (2, 4), (3, 5))[step]
    return turn * TURN + first, turn * TURN + second


def transpose_words(nc, bank, rows_bf16, ident):
    words = rows_bf16.bitcast(F32)
    for u in range(HALVES):
        nc.tensor.transpose(bank[:, u, :], words[:, u * P : (u + 1) * P], ident[:])


def tile_gatedmemorymodule_pa_kernel(tc, queries, memory_items, out):
    nc = tc.nc
    with tc.tile_pool(name="keep", bufs=1) as keep, tc.tile_pool(name="late_loads", bufs=4) as late_loads, tc.tile_pool(
        name="stage2", bufs=2
    ) as stage2, tc.psum_pool(name="psum_t", bufs=4) as psum_t, tc.psum_pool(name="psum_s", bufs=4) as psum_s, tc.manual_schedule():
        warm = keep.tile([P, 1], F32)
        nc.vector.memset(warm[:], 0.0)
        nc.scalar.activation(out=warm[:], in_=warm[:], func=ACT.Exp)

        ident = keep.tile([P, P], F32)
        make_identity(nc, ident[:])
        ident_bf16 = keep.tile([P, P], BF16)
        make_identity(nc, ident_bf16[:])

        scores = keep.tile([P, CHUNKS, M, PACK], F32)
        q2_codes = keep.tile([P, CHUNKS, D], U32, align_bytes=64)
        q2_scales = keep.tile([P, CHUNKS, D], U8, align_bytes=64)
        mem_codes = keep.tile([P, M], U32, align_bytes=64)
        mem_scales = keep.tile([P, M], U8, align_bytes=64)
        neg_max = keep.tile([P, M], BF16)

        raw = {}
        q2_grouped = {}
        interleaved = {}

        def load(c, pool, pieces=1, tag="raw", bufs=None):
            raw[c] = pool.tile([P, PACK, D], BF16, name="raw", tag=tag, bufs=bufs)
            steps = PACK // pieces
            for i in range(0, PACK, steps):
                nc.sync.dma_start(
                    out=raw[c][:, i : i + steps],
                    in_=queries[c * PACK + i : c * PACK + i + steps].rearrange("t b d -> b t d"),
                )

        def load_late(c):
            load(c, late_loads, tag="raw_late", bufs=4)

        def grouped(c):
            if c - c % 2 not in q2_grouped:
                q2_grouped[c - c % 2] = stage2.tile([P, 2, D, PACK], BF16, align_bytes=64, name="q2_grouped")
            return q2_grouped[c - c % 2][:, c % 2]

        def regroup(c, copy, columns):
            copy(
                out=grouped(c)[:, columns, :].rearrange("p (c i) t -> p c t i", i=4),
                in_=raw[c][:, :, columns].rearrange("p t (c i) -> p c t i", i=4),
            )

        def quantise_q2(c):
            nc.vector.quantize_mx(
                out=q2_codes[:, c : c + 2, :].rearrange("p c d -> p (c d)").bitcast(FP8X4),
                scales=q2_scales[:, c : c + 2, :].rearrange("p c d -> p (c d)"),
                in_=q2_grouped[c][:].rearrange("p c d t -> p (c d t)"),
            )

        def interleave_on_tensor(c, half, pool, tag):
            bank = pool.tile([P, D // 2, PACK], BF16, tag=tag, name="interleaved")
            columns = slice(half * D // 2, (half + 1) * D // 2)
            for t in range(0, PACK, 2):
                nc.tensor.matmul(
                    out=bank[:, :, t : t + 2],
                    lhsT=ident_bf16[:],
                    rhs=raw[c][:, t : t + 2, columns].rearrange("p t d -> p d t"),
                    start=True,
                    stop=True,
                )
            interleaved[c, half] = bank

        def take_interleaved(c, half):
            nc.scalar.copy(
                out=grouped(c)[:, half * D // 2 : (half + 1) * D // 2, :],
                in_=interleaved[c, half][:],
            )

        with tc.tile_pool(name="loads", bufs=5) as loads, tc.tile_pool(name="stage1", bufs=2) as stage1:
            turn_min = stage1.tile([P, 3, M, PACK], BF16, bufs=1)
            running_min = stage1.tile([P, 3, M, PACK], BF16, bufs=1)
            banks = {}
            q1_grouped = {}
            score_bank = {}

            def transposes(c):
                banks[c] = []
                for pair in range(PACK // 2):
                    bank = psum_t.tile([P, 2, HALVES, B], F32, tag="bank", name="bank")
                    for i in range(2):
                        transpose_words(nc, bank[:, i], raw[c][:, 2 * pair + i, :], ident)
                    banks[c].append(bank)

            def copy_out(r, half):
                if half == 0:
                    q1_grouped[r] = stage1.tile([P, 2, PACK, B, PACK], BF16, align_bytes=64, name="q1_grouped")
                q1_words = q1_grouped[r][:, half].bitcast(F32)
                for pair in range(PACK // 2):
                    nc.scalar.copy(
                        out=q1_words[:, 2 * pair : 2 * pair + 2],
                        in_=banks[round_chunks(r)[half]][pair][:].rearrange("p i u b -> p i b u"),
                    )

            def first_product(r):
                codes = stage1.tile([P, 2, PACK * B], U32, align_bytes=64, name="q1_codes")
                scales = stage1.tile([P, 2, PACK * B], U8, align_bytes=64, name="q1_scales")
                nc.vector.quantize_mx(
                    out=codes[:].rearrange("p c r -> p (c r)").bitcast(FP8X4),
                    scales=scales[:].rearrange("p c r -> p (c r)"),
                    in_=q1_grouped[r][:].rearrange("p c t b k -> p (c t b k)"),
                )
                for half in range(2):
                    bank = psum_s.tile([P, PACK, M], F32, name="score_bank")
                    score_bank[round_chunks(r)[half]] = bank
                    for j in range(PACK):
                        nc.tensor.matmul_mx(
                            out=bank[:, j, :],
                            lhsT=codes[:, half, j * B : (j + 1) * B].bitcast(FP8X4),
                            lhsT_scale=scales[:, half, j * B : (j + 1) * B],
                            rhs=mem_codes[:].bitcast(FP8X4),
                            rhs_scale=mem_scales[:],
                            start=True,
                            stop=True,
                        )

            def keep_scores(c):
                nc.scalar.mul(out=scores[:, c], in_=score_bank[c][:].rearrange("p j m -> p m j"), mul=-1.0 / TEMP)

            def minimum(out, in0, in1):
                nc.vector.tensor_tensor(out=out, in0=in0, in1=in1, op=ALU.min)

            def minimum_of_turn(turn):
                c = turn * TURN
                minimum((turn_min if turn else running_min)[:], scores[:, c : c + 3], scores[:, c + 3 : c + 6])

            def load_round(r):
                for c in round_chunks(r):
                    if c % TURN == 1:
                        load(c, loads, tag="raw_scalar", bufs=2)
                    else:
                        load(c, loads, tag="raw", bufs=5)

            def scalars_third(step):
                turn, third = divmod(step, 3)
                if turn > 0:
                    chunk = turn * TURN + (0 if turn == ROUNDS // 3 else 1)
                    regroup(chunk, nc.scalar.copy, THIRDS[third])

            load(0, loads, pieces=2, tag="raw", bufs=5)
            mem_raw = late_loads.tile([P, D], BF16, tag="raw_late", bufs=4, name="mem_raw")
            nc.sync.dma_start(out=mem_raw[:], in_=memory_items)
            load(1, loads, tag="raw_scalar", bufs=2)
            for r in range(1, AHEAD):
                load_round(r)
            transposes(round_chunks(0)[0])
            regroup(round_chunks(0)[0], nc.vector.tensor_copy, ALL_COLUMNS)
            mem_bank = psum_s.tile([P, HALVES, M], F32, name="mem_bank", tag="score_bank")
            transpose_words(nc, mem_bank, mem_raw[:], ident)
            mem_grouped = stage1.tile([P, M, PACK], BF16, align_bytes=64, bufs=1)
            nc.vector.tensor_copy(out=mem_grouped[:].bitcast(F32), in_=mem_bank[:].rearrange("p u m -> p m u"))
            nc.vector.quantize_mx(
                out=mem_codes[:].bitcast(FP8X4),
                scales=mem_scales[:],
                in_=mem_grouped[:].rearrange("p m k -> p (m k)"),
            )

            for r in range(ROUNDS + 2):
                if r + AHEAD < ROUNDS:
                    load_round(r + AHEAD)
                if r == ROUNDS - AHEAD:
                    for c in AT_THE_BARRIER + BESIDE_EXP[:1]:
                        load(c, late_loads, tag="raw_late", bufs=4)
                if r < ROUNDS:
                    transposes(round_chunks(r)[1])
                    copy_out(r, 0)
                if r + 1 < ROUNDS:
                    transposes(round_chunks(r + 1)[0])
                if 2 <= r <= ROUNDS:
                    keep_scores(round_chunks(r - 2)[0])
                if r < ROUNDS:
                    copy_out(r, 1)
                if 2 <= r <= ROUNDS:
                    keep_scores(round_chunks(r - 2)[1])
                if 1 <= r <= ROUNDS:
                    first_product(r - 1)
                if 5 <= r < ROUNDS and r % 3 == 2:
                    minimum_of_turn(r // 3 - 1)
                if 3 <= r <= ROUNDS and r % 3 == 0:
                    quantise_q2((r // 3 - 1) * TURN)
                if 4 <= r and r % 3 == 1:
                    quantise_q2((r // 3 - 1) * TURN + 2)
                if r == ROUNDS:
                    minimum_of_turn(r // 3 - 1)
                scalars_third(r)
                if r == ROUNDS:
                    for c in round_chunks(r - 1):
                        keep_scores(c)
                if r == 0:
                    regroup(round_chunks(r)[1], nc.vector.tensor_copy, ALL_COLUMNS)
                if 0 < r < ROUNDS - 1:
                    regroup(round_chunks(r)[0], nc.vector.tensor_copy, ALL_COLUMNS)
                if 8 < r <= ROUNDS and r % 3 == 0:
                    minimum(running_min[:], running_min[:], turn_min[:])
            minimum(running_min[:], running_min[:], turn_min[:])
            minimum(running_min[:, 0], running_min[:, 0], running_min[:, 1])
            minimum(turn_min[:, 0], scores[:, CHUNKS - 2], scores[:, CHUNKS - 1])
            minimum(running_min[:, 0], running_min[:, 0], running_min[:, 2])
            minimum(running_min[:, 0], running_min[:, 0], turn_min[:, 0])
            nc.vector.tensor_reduce(out=neg_max[:], in_=running_min[:, 0], axis=AXIS.X, op=ALU.min)

        load(CHUNKS - 1, late_loads, tag="raw_late", bufs=4)
        regroup(AT_THE_BARRIER[0], nc.scalar.copy, ALL_COLUMNS)
        regroup(AT_THE_BARRIER[1], nc.scalar.copy, slice(0, D // 2))
        load(BESIDE_EXP[1], late_loads, tag="raw_late", bufs=4)

        with tc.tile_pool(name="soft", bufs=1) as soft:
            q2_grouped[AT_THE_END[0]] = soft.tile([P, 2, D, PACK], BF16, align_bytes=64, name="last_grouped")
            total = soft.tile([P, M], F32)
            inverse = soft.tile([P, M], F32)
            v_att = soft.tile([P, CHUNKS, M, PACK], BF16, align_bytes=64)
            v_codes = soft.tile([P, CHUNKS, M], U32, align_bytes=64)
            v_scales = soft.tile([P, CHUNKS, M], U8, align_bytes=64)

            def normalise(slots, first, count):
                part = slice(first, first + count)
                nc.vector.tensor_tensor(
                    out=v_att[:, part, slots, :],
                    in0=scores[:, part, slots, :],
                    in1=inverse[:, slots].unsqueeze(1).unsqueeze(3).to_broadcast([P, count, slots.stop - slots.start, PACK]),
                    op=ALU.mult,
                )

            def quantise_v(first, count):
                part = slice(first, first + count)
                nc.vector.quantize_mx(
                    out=v_codes[:, part, :].rearrange("p c m -> p (c m)").bitcast(FP8X4),
                    scales=v_scales[:, part, :].rearrange("p c m -> p (c m)"),
                    in_=v_att[:, part].rearrange("p c m t -> p (c m t)"),
                )

            def vector_late(g):
                if g == 0:
                    regroup(CHUNKS - 1, nc.vector.tensor_copy, ALL_COLUMNS)
                    regroup(AT_THE_BARRIER[1], nc.vector.tensor_copy, slice(D // 2, D))
                    quantise_q2(CHUNKS - 2)
                    for c in BESIDE_EXP:
                        regroup(c, nc.vector.tensor_copy, ALL_COLUMNS)
                    quantise_q2(AT_THE_BARRIER[0])
                if g == 1:
                    quantise_q2(BESIDE_EXP[0])
                    regroup(AT_THE_END[0], nc.vector.tensor_copy, ALL_COLUMNS)

            after_exp = [(c, half) for c in AFTER_EXP for half in range(2)]
            first_slot = 0
            for g, count in enumerate(SLOT_GROUPS):
                slots = slice(first_slot, first_slot + count)
                first_slot += count
                for m in range(slots.start, slots.stop):
                    nc.scalar.activation(
                        out=scores[:, :, m, :],
                        in_=scores[:, :, m, :],
                        func=ACT.Exp,
                        bias=neg_max[:, m : m + 1],
                        scale=-1.0,
                        accum_out=total[:, m : m + 1],
                    )
                vector_late(g)
                if g == 0:
                    for c in (AT_THE_END[0], *AFTER_EXP[0:2], AT_THE_END[1]):
                        load(c, late_loads, tag="raw_late", bufs=4)
                if g == 1:
                    for c, half in after_exp[:4]:
                        interleave_on_tensor(c, half, psum_t, "bank")
                    for c in AFTER_EXP[2:4]:
                        load(c, late_loads, tag="raw_late", bufs=4)
                if g == 2:
                    for c, half in after_exp[4:7]:
                        interleave_on_tensor(c, half, psum_s, "score_bank")
                if g == len(SLOT_GROUPS) - 1:
                    take_interleaved(*after_exp[0])
                    interleave_on_tensor(*after_exp[7], psum_t, "bank")
                nc.vector.reciprocal(out=inverse[:, slots], in_=total[:, slots])
                if g < len(SLOT_GROUPS) - 1:
                    normalise(slots, 0, CHUNKS)

            acc = psum_s.tile([P, D], F32, tag="score_bank", name="acc")
            for n in range(WARM_UPS):
                nc.tensor.matmul(
                    out=acc[:, : slots.start * PACK],
                    lhsT=ident_bf16[:],
                    rhs=v_att[:, 0, : slots.start, :].rearrange("p m t -> p (m t)"),
                    start=True,
                    stop=True,
                )

            def second_product(c, start, stop):
                nc.tensor.matmul_mx(
                    out=acc[:],
                    lhsT=v_codes[:, c, :].bitcast(FP8X4),
                    lhsT_scale=v_scales[:, c, :],
                    rhs=q2_codes[:, c, :].bitcast(FP8X4),
                    rhs_scale=q2_scales[:, c, :],
                    start=start,
                    stop=stop,
                )

            for c, half in after_exp[1:]:
                take_interleaved(c, half)
            regroup(AT_THE_END[1], nc.scalar.copy, ALL_COLUMNS)
            normalise(slots, 0, WIDE)
            normalise(slots, WIDE, WIDE)
            quantise_v(0, WIDE // 2)
            normalise(slots, 2 * WIDE, 2 * WIDE)
            quantise_v(WIDE // 2, WIDE // 2)
            for first in range(WIDE, CHUNKS, WIDE):
                quantise_v(first, WIDE)
            for c in (*AFTER_EXP[::2], AT_THE_END[0]):
                quantise_q2(c)
            last = AFTER_EXP + AT_THE_END
            order = [c for c in range(CHUNKS) if c not in last] + last
            for c in order:
                second_product(c, start=(c == order[0]), stop=(c == order[-1]))
            result = late_loads.tile([P, D], F32, tag="raw_late", bufs=4, name="result")
            nc.scalar.mul(out=result[:], in_=acc[:], mul=1.0 / B)
            nc.sync.dma_start(out=out, in_=result[:])
